import numpy as np
import ml_dtypes


def mxq(x, axis, fmt="e4m3"):
    dtype, down = {"e4m3": (ml_dtypes.float8_e4m3fn, 7), "e5m2": (ml_dtypes.float8_e5m2, 14)}[fmt]
    v = np.moveaxis(np.asarray(x, np.float32).astype(ml_dtypes.bfloat16).astype(np.float64), axis, -1)
    blocks = v.reshape(v.shape[:-1] + (-1, 32))
    amax = np.abs(blocks).max(-1, keepdims=True)
    byte = np.maximum(np.where(amax > 0, np.frexp(amax)[1] - 1 + 127, 0) - down, 1)
    scale = np.exp2(byte - 127.0)
    codes = (blocks / scale).astype(np.float32).astype(dtype).astype(np.float64)
    return np.moveaxis((codes * scale).reshape(v.shape), -1, axis)


WIDE = False


def mx_kscale(k):
    if not WIDE:
        return np.ones(k)
    levels = np.array([10, -10, 5, -5, 0])
    a = np.random.permutation(np.resize(levels, k // 512 * 4)).reshape(k // 512, 4)
    idx = np.arange(k)
    return np.exp2(a[idx // 512, idx % 128 // 32])


BF16 = ml_dtypes.bfloat16


def bf(x):
    return np.asarray(x, np.float32).astype(BF16)


def f64(x):
    return np.asarray(x).astype(np.float64)


B, DIM, HID, LS = 256, 128, 512, 63
DL = DIM * LS
O1 = DL
O2 = O1 + DL
O3 = O2 + DL
O4 = O3 + DIM
O5 = O4 + DIM
P = O5 + DIM


def elu(v):
    return np.where(v > 0.0, v, np.exp(np.minimum(v, 0.0)) - 1.0)


def sigmoid(v):
    return 1.0 / (1.0 + np.exp(-v))


def col_scale():
    return np.concatenate([np.full(DL, 0.5), np.full(DL, 1.0), np.full(DL, 2.5 / np.sqrt(LS)),
                           np.full(DIM, 0.5), np.full(DIM, 8.0), np.full(DIM, 2.5)])


def setup_inputs():
    t = mx_kscale(HID)
    cs = col_scale()
    return {"x": bf(np.random.standard_normal((B, DIM))),
            "cond": bf(np.random.standard_normal((B, DIM))),
            "W1": bf(np.random.standard_normal((DIM, HID)) / np.sqrt(DIM) * t),
            "b1": bf(np.random.standard_normal(HID) * 0.5 * t),
            "W2": bf(np.random.standard_normal((HID, P)) * 1.2 / np.sqrt(HID) * cs / t[:, None]),
            "b2": bf(np.random.standard_normal(P) * 0.5 * cs)}


def reference(x, cond, W1, b1, W2, b2):
    x = f64(x)
    h = np.maximum(f64(cond) @ f64(W1) + f64(b1), 0.0)
    p = (mxq(h, 1, "e4m3") @ mxq(f64(W2), 0, "e4m3")) + f64(b2)
    n = x.shape[0]
    mat1 = p[:, :O1].reshape(n, DIM, LS)
    bias1 = p[:, O1:O2].reshape(n, DIM, LS)
    mat2 = p[:, O2:O3].reshape(n, DIM, LS)
    bias2 = p[:, O3:O4]
    eps = p[:, O4:O5] / 10.0
    alpha = p[:, O5:] / 10.0
    z = x[:, :, None] * mat1 + bias1
    num = np.sum(elu(z) * mat2, axis=-1)
    den = np.sum(np.maximum(-mat1 * mat2, 0.0), axis=-1) + 1.0
    return np.exp(alpha) * (x + 0.8 * sigmoid(eps) * num / den) + bias2

@@ -1,0 +1,370 @@
+from contextlib import ExitStack
+
+import concourse.mybir as mybir
+from concourse.masks import make_identity
+
+F32 = mybir.dt.float32
+BF16 = mybir.dt.bfloat16
+U32 = mybir.dt.uint32
+U8 = mybir.dt.uint8
+FP8X4 = mybir.dt.float8_e4m3fn_x4
+ALU = mybir.AluOpType
+ACT = mybir.ActivationFunctionType
+
+P = 128
+PACK = 4
+BATCH = 256
+HALVES = BATCH // P
+DIM = 128
+HID = 512
+LS = 63
+DL = DIM * LS
+SECTIONS = 3
+TAIL0 = SECTIONS * DL
+PAIR_COLS = 2 * LS
+TILES = DIM // 2
+PAIRS = TILES // 2
+STEP_COLS = 2 * PAIR_COLS
+CHUNK_PAIRS = 4
+CHUNKS = PAIRS // CHUNK_PAIRS
+CHUNK_COLS = CHUNK_PAIRS * STEP_COLS
+GROUPED_BUFS = 3
+
+FLOPS = 2 * BATCH * DIM * HID + 2 * BATCH * HID * (TAIL0 + 3 * DIM)
+
+
+def tile_cn_pa_kernel(tc, x, cond, W1, b1, W2, b2, out):
+    nc = tc.nc
+    with ExitStack() as ctx:
+        const = ctx.enter_context(tc.tile_pool(name="const", bufs=1))
+        raw_pool = ctx.enter_context(tc.tile_pool(name="raw", bufs=6))
+        mx_pool = ctx.enter_context(tc.tile_pool(name="mx", bufs=3))
+        work = ctx.enter_context(tc.tile_pool(name="work", bufs=3))
+
+        x_sb = const.tile([P, HALVES, DIM], BF16)
+        cond_sb = const.tile([P, HALVES, DIM], BF16)
+        w1_sb = const.tile([P, HID], BF16)
+        b1_sb = const.tile([P, PACK], BF16)
+        b2_rows_a = const.tile([P, P], BF16)
+        b2_rows_b = const.tile([P, P], BF16)
+        b2_tail = const.tile([P, 3 * DIM], BF16)
+        nc.vector.memset(b2_rows_a[:], 0.0)
+        nc.vector.memset(b2_rows_b[:], 0.0)
+        with nc.allow_non_contiguous_dma(reason="small inputs, loaded once"):
+            nc.scalar.dma_start(out=cond_sb[:], in_=cond.rearrange("(h p) d -> p h d", p=P))
+            nc.scalar.dma_start(out=w1_sb[:], in_=W1)
+            nc.scalar.dma_start(out=b1_sb[:], in_=b1.rearrange("(p j) -> p j", j=PACK))
+            nc.scalar.dma_start(out=x_sb[:], in_=x.rearrange("(h p) d -> p h d", p=P))
+            nc.scalar.dma_start(
+                out=b2_rows_a[:, 0:PAIR_COLS],
+                in_=b2[0 : P * PAIR_COLS].rearrange("(r m) -> r m", m=PAIR_COLS),
+            )
+            nc.scalar.dma_start(
+                out=b2_rows_b[0:TILES, 0:PAIR_COLS],
+                in_=b2[P * PAIR_COLS : TAIL0].rearrange("(r m) -> r m", m=PAIR_COLS),
+            )
+            nc.scalar.dma_start(out=b2_tail[:], in_=b2[TAIL0 : TAIL0 + 3 * DIM].partition_broadcast(P))
+
+        ident = const.tile([P, P], BF16)
+        make_identity(nc, ident[:])
+
+        spread = const.tile([P, DL + 2], BF16)
+        nc.gpsimd.memset(spread[:, DL : DL + 2], 0.0)
+        feats = DIM // CHUNKS
+        for g in range(CHUNKS):
+            nc.gpsimd.tensor_scalar(
+                out=spread[:, g * CHUNK_COLS : (g + 1) * CHUNK_COLS].rearrange("p (d l) -> p d l", l=LS),
+                in0=ident[:, g * feats : (g + 1) * feats].unsqueeze(2).to_broadcast([P, feats, LS]),
+                scalar1=1.0,
+                scalar2=0.0,
+                op0=ALU.mult,
+                op1=ALU.add,
+            )
+
+        x_t = const.tile([P, BATCH], BF16)
+        cond_t = const.tile([P, BATCH], BF16)
+        bias_t = const.tile([P, SECTIONS, TILES], F32)
+        pick = const.tile([P, 2], F32)
+        b1_f = const.tile([P, PACK], F32)
+        x_f = const.tile([P, HALVES, DIM], F32)
+        h_grouped = const.tile([P, BATCH, PACK], BF16, align_bytes=64)
+        h_codes = const.tile([P, BATCH], U32, align_bytes=64)
+        h_scales = const.tile([P, BATCH], U8, align_bytes=64)
+        minus_one = const.tile([P, 1], F32)
+        nc.vector.memset(minus_one[:], -1.0)
+        nc.vector.tensor_copy(out=b1_f[:], in_=b1_sb[:])
+        nc.vector.tensor_copy(out=x_f[:], in_=x_sb[:])
+
+        with tc.psum_pool(name="psum_start", bufs=1) as psum_start:
+            cond_t_ps = psum_start.tile([P, BATCH], BF16)
+            x_t_ps = psum_start.tile([P, BATCH], BF16)
+            for h in range(HALVES):
+                nc.tensor.transpose(cond_t_ps[:, h * P : (h + 1) * P], cond_sb[:, h, :], ident[:])
+            nc.vector.tensor_copy(out=cond_t[:], in_=cond_t_ps[:])
+            for h in range(HALVES):
+                nc.tensor.transpose(x_t_ps[:, h * P : (h + 1) * P], x_sb[:, h, :], ident[:])
+            nc.vector.tensor_copy(out=x_t[:], in_=x_t_ps[:])
+
+            w1_by_j = w1_sb[:].rearrange("k (p j) -> k j p", j=PACK)
+            h_ps = [
+                psum_start.tile([P, 2, BATCH], F32, name="h_ps0"),
+                psum_start.tile([P, 2, BATCH], F32, name="h_ps1"),
+            ]
+            for j in range(PACK):
+                nc.tensor.matmul(
+                    out=h_ps[j // 2][:, j % 2, :], lhsT=w1_by_j[:, j, :], rhs=cond_t[:], start=True, stop=True
+                )
+            for j in range(PACK):
+                nc.scalar.activation(
+                    out=h_grouped[:, :, j],
+                    in_=h_ps[j // 2][:, j % 2, :],
+                    func=ACT.Relu,
+                    bias=b1_f[:, j : j + 1],
+                    scale=1.0,
+                )
+            nc.vector.quantize_mx(
+                out=h_codes[:].bitcast(FP8X4),
+                scales=h_scales[:],
+                in_=h_grouped[:].rearrange("p b j -> p (b j)"),
+            )
+
+            bias_t_ps = psum_start.tile([P, 2 * P], BF16)
+            nc.tensor.transpose(bias_t_ps[:, 0:P], b2_rows_a[:], ident[:])
+            nc.tensor.transpose(bias_t_ps[:, P : 2 * P], b2_rows_b[:], ident[:])
+            nc.vector.tensor_copy(
+                out=bias_t[:].rearrange("p s c -> p (s c)"), in_=bias_t_ps[:, 0 : SECTIONS * TILES]
+            )
+            nc.vector.tensor_scalar_add(out=bias_t[:, 1, :], in0=bias_t[:, 1, :], scalar1=1.0)
+
+            pick_ps = psum_start.tile([P, P], BF16)
+            nc.tensor.transpose(pick_ps[:], spread[:, 0:P], ident[:])
+            nc.vector.tensor_copy(out=pick[:], in_=pick_ps[:, 0:2])
+
+        psum = ctx.enter_context(tc.psum_pool(name="psum", bufs=2))
+        psum_one = ctx.enter_context(tc.psum_pool(name="psum_one", bufs=1))
+
+        grouped_tiles = []
+        for i in range(GROUPED_BUFS):
+            grouped = const.tile([P, SECTIONS, 2, P, PACK], BF16, name="grouped%d" % i, align_bytes=64)
+            nc.vector.memset(grouped[:, :, :, P - 16 : P, :], 0.0)
+            grouped_tiles.append(grouped)
+
+        w2_by_p = W2.rearrange("(p j) c -> p j c", j=PACK)
+
+        sums = psum_one.tile([P, 2, HALVES, DIM], F32)
+
+        tail_raw = const.tile([P, PACK, 3 * DIM], BF16)
+        tail_grouped = const.tile([P, 3 * DIM, PACK], BF16, align_bytes=64)
+        tail_codes = const.tile([P, 3 * DIM], U32, align_bytes=64)
+        tail_scales = const.tile([P, 3 * DIM], U8, align_bytes=64)
+        tail = const.tile([P, HALVES, 3, DIM], F32)
+
+        raws = []
+
+        def load_chunk(g):
+            raws.append([])
+            for s in range(SECTIONS):
+                raw = raw_pool.tile([P, PACK, CHUNK_COLS], BF16, name="raw")
+                col0 = s * DL + g * CHUNK_COLS
+                nc.sync.dma_start(out=raw[:], in_=w2_by_p[:, :, col0 : col0 + CHUNK_COLS])
+                raws[g].append(raw)
+
+        codes_of, scales_of, p_ps_of, x_e_ps_of, x_e_of = [], [], [], [], []
+        mat2_of, z1_of, m1m2_of, ez_of, num_of, den_of = [], [], [], [], [], []
+
+        def regroup(n):
+            grouped = grouped_tiles[n % GROUPED_BUFS]
+            first = (n % CHUNK_PAIRS) * STEP_COLS
+            for s in range(SECTIONS):
+                src = raws[n // CHUNK_PAIRS][s][:, :, first : first + STEP_COLS].rearrange(
+                    "p j (t w) -> p t w j", w=PAIR_COLS
+                )
+                if s < 2:
+                    nc.scalar.copy(out=grouped[:, s, :, 0:PAIR_COLS, :], in_=src)
+                else:
+                    nc.vector.tensor_copy(out=grouped[:, s, :, 0:PAIR_COLS, :], in_=src)
+
+        def quantise(n):
+            grouped = grouped_tiles[n % GROUPED_BUFS]
+            codes = mx_pool.tile([P, SECTIONS, 2 * P], U32, name="codes", align_bytes=64)
+            scales = mx_pool.tile([P, SECTIONS, 2 * P], U8, name="scales", align_bytes=64)
+            for s in range(SECTIONS):
+                nc.vector.quantize_mx(
+                    out=codes[:, s, :].bitcast(FP8X4),
+                    scales=scales[:, s, :],
+                    in_=grouped[:, s, :, :, :].rearrange("p t w j -> p (t w j)"),
+                )
+            codes_of.append(codes)
+            scales_of.append(scales)
+
+        def multiply(n):
+            p_ps = [psum.tile([P, 2, BATCH], F32, name="p_ps%d" % s) for s in range(SECTIONS)]
+            for u in range(2):
+                cols = slice(u * P, (u + 1) * P)
+                for s in range(SECTIONS):
+                    nc.tensor.matmul_mx(
+                        out=p_ps[s][:, u, :],
+                        lhsT=codes_of[n][:, s, cols].bitcast(FP8X4),
+                        lhsT_scale=scales_of[n][:, s, cols],
+                        rhs=h_codes[:].bitcast(FP8X4),
+                        rhs_scale=h_scales[:],
+                        start=True,
+                        stop=True,
+                    )
+            x_e_ps = psum_one.tile([P, 2, BATCH], BF16, name="x_e_ps", tag="misc")
+            for u in range(2):
+                c = 2 * n + u
+                nc.tensor.matmul(
+                    out=x_e_ps[:, u, :],
+                    lhsT=spread[:, c * PAIR_COLS : c * PAIR_COLS + P],
+                    rhs=x_t[:],
+                    start=True,
+                    stop=True,
+                )
+            p_ps_of.append(p_ps)
+            x_e_ps_of.append(x_e_ps)
+
+        def fetch(n):
+            mat2 = work.tile([P, 2, BATCH], F32, name="mat2")
+            x_e = work.tile([P, 2, BATCH], BF16, name="x_e")
+            for u in range(2):
+                c = 2 * n + u
+                nc.scalar.activation(
+                    out=mat2[:, u, :], in_=p_ps_of[n][2][:, u, :], func=ACT.Identity,
+                    bias=bias_t[:, 2, c : c + 1], scale=1.0,
+                )
+            nc.scalar.copy(out=x_e[:], in_=x_e_ps_of[n][:])
+            mat2_of.append(mat2)
+            x_e_of.append(x_e)
+
+        def products(n):
+            xm1 = work.tile([P, 2, BATCH], F32, name="xm1")
+            z1 = work.tile([P, 2, BATCH], F32, name="z1")
+            m1m2 = work.tile([P, 2, BATCH], F32, name="m1m2")
+            p_ps = p_ps_of[n]
+            for u in range(2):
+                c = 2 * n + u
+                nc.vector.scalar_tensor_tensor(
+                    out=xm1[:, u, :], in0=p_ps[0][:, u, :], scalar=bias_t[:, 0, c : c + 1],
+                    in1=x_e_of[n][:, u, :], op0=ALU.add, op1=ALU.mult,
+                )
+                nc.vector.scalar_tensor_tensor(
+                    out=m1m2[:, u, :], in0=p_ps[0][:, u, :], scalar=bias_t[:, 0, c : c + 1],
+                    in1=mat2_of[n][:, u, :], op0=ALU.add, op1=ALU.mult,
+                )
+                nc.vector.scalar_tensor_tensor(
+                    out=z1[:, u, :], in0=p_ps[1][:, u, :], scalar=bias_t[:, 1, c : c + 1],
+                    in1=xm1[:, u, :], op0=ALU.add, op1=ALU.add,
+                )
+            z1_of.append(z1)
+            m1m2_of.append(m1m2)
+
+        def functions(n):
+            ez = work.tile([P, 2, BATCH], F32, name="ez")
+            den_terms = work.tile([P, 2, BATCH], F32, name="den_terms")
+            nc.scalar.activation(out=ez[:], in_=z1_of[n][:], func=ACT.Exp, bias=minus_one[:], scale=1.0)
+            nc.scalar.activation(out=den_terms[:], in_=m1m2_of[n][:], func=ACT.Relu, scale=-1.0)
+            ez_of.append(ez)
+            den_of.append(den_terms)
+
+        def elu_terms(n):
+            elu1 = work.tile([P, 2, BATCH], F32, name="elu1")
+            num_terms = work.tile([P, 2, BATCH], F32, name="num_terms")
+            nc.vector.scalar_tensor_tensor(
+                out=elu1[:], in0=ez_of[n][:], scalar=1.0, in1=z1_of[n][:], op0=ALU.min, op1=ALU.max
+            )
+            nc.vector.scalar_tensor_tensor(
+                out=num_terms[:], in0=elu1[:], scalar=-1.0, in1=mat2_of[n][:], op0=ALU.add, op1=ALU.mult
+            )
+            num_of.append(num_terms)
+
+        def add_up(n):
+            for u in range(2):
+                c = 2 * n + u
+                for h in range(HALVES):
+                    samples = slice(h * P, (h + 1) * P)
+                    for kind, terms in enumerate((num_of[n], den_of[n])):
+                        nc.tensor.matmul(
+                            out=sums[:, kind, h, 2 * c : 2 * c + 2],
+                            lhsT=terms[:, u, samples],
+                            rhs=pick[:],
+                            start=True,
+                            stop=True,
+                        )
+
+        def run(stage, n):
+            if 0 <= n < PAIRS:
+                stage(n)
+
+        load_chunk(0)
+        nc.sync.dma_start(out=tail_raw[:], in_=w2_by_p[:, :, TAIL0 : TAIL0 + 3 * DIM])
+        nc.vector.tensor_copy(out=tail_grouped[:], in_=tail_raw[:].rearrange("p j w -> p w j"))
+        for i in range(3):
+            cols = slice(i * DIM, (i + 1) * DIM)
+            nc.vector.quantize_mx(
+                out=tail_codes[:, cols].bitcast(FP8X4),
+                scales=tail_scales[:, cols],
+                in_=tail_grouped[:, cols, :].rearrange("p w j -> p (w j)"),
+            )
+        for h in range(HALVES):
+            samples = slice(h * P, (h + 1) * P)
+            tail_ps = psum_one.tile([P, 3, DIM], F32, name="tail_ps", tag="misc")
+            for i in range(3):
+                cols = slice(i * DIM, (i + 1) * DIM)
+                nc.tensor.matmul_mx(
+                    out=tail_ps[:, i, :],
+                    lhsT=h_codes[:, samples].bitcast(FP8X4),
+                    lhsT_scale=h_scales[:, samples],
+                    rhs=tail_codes[:, cols].bitcast(FP8X4),
+                    rhs_scale=tail_scales[:, cols],
+                    start=True,
+                    stop=True,
+                )
+            nc.vector.tensor_tensor(
+                out=tail[:, h, :, :].rearrange("p i d -> p (i d)"),
+                in0=tail_ps[:].rearrange("p i d -> p (i d)"),
+                in1=b2_tail[:],
+                op=ALU.add,
+            )
+        exp_alpha = const.tile([P, HALVES, DIM], F32)
+        gate_den = const.tile([P, HALVES, DIM], F32)
+        base = const.tile([P, HALVES, DIM], F32)
+        nc.scalar.activation(out=exp_alpha[:], in_=tail[:, :, 2, :], func=ACT.Exp, scale=0.1)
+        nc.scalar.activation(out=gate_den[:], in_=tail[:, :, 1, :], func=ACT.Exp, scale=-0.1)
+        nc.vector.tensor_scalar_add(out=gate_den[:], in0=gate_den[:], scalar1=1.0)
+        nc.vector.tensor_tensor(out=base[:], in0=exp_alpha[:], in1=x_f[:], op=ALU.mult)
+        nc.vector.tensor_tensor(out=base[:], in0=base[:], in1=tail[:, :, 0, :], op=ALU.add)
+
+        load_chunk(1)
+
+        with tc.manual_schedule():
+            for step in range(PAIRS + 5):
+                run(functions, step - 4)
+                run(fetch, step - 3)
+                run(quantise, step - 1)
+                run(regroup, step)
+                if step % CHUNK_PAIRS == CHUNK_PAIRS - 1 and step // CHUNK_PAIRS + 2 < CHUNKS:
+                    load_chunk(step // CHUNK_PAIRS + 2)
+                run(elu_terms, step - 4)
+                run(products, step - 3)
+                run(multiply, step - 2)
+                run(add_up, step - 5)
+
+        flat = "p h d -> p (h d)"
+        divisor = const.tile([P, HALVES, DIM], F32)
+        result = const.tile([P, HALVES, DIM], F32)
+        nc.vector.scalar_tensor_tensor(
+            out=divisor[:].rearrange(flat), in0=sums[:, 1, :, :].rearrange(flat), scalar=1.0,
+            in1=gate_den[:].rearrange(flat), op0=ALU.add, op1=ALU.mult,
+        )
+        nc.vector.reciprocal(out=divisor[:], in_=divisor[:])
+        nc.vector.tensor_tensor(
+            out=result[:].rearrange(flat), in0=sums[:, 0, :, :].rearrange(flat),
+            in1=divisor[:].rearrange(flat), op=ALU.mult,
+        )
+        nc.vector.scalar_tensor_tensor(
+            out=result[:].rearrange(flat), in0=result[:].rearrange(flat), scalar=0.8,
+            in1=exp_alpha[:].rearrange(flat), op0=ALU.mult, op1=ALU.mult,
+        )
+        nc.vector.tensor_tensor(out=result[:], in0=result[:], in1=base[:], op=ALU.add)
+        nc.sync.dma_start(out=out.rearrange("(h p) d -> p h d", p=P), in_=result[:])

@@ -25,9 +25,7 @@ PAIR_COLS = 2 * LS
 TILES = DIM // 2
 PAIRS = TILES // 2
 STEP_COLS = 2 * PAIR_COLS
-CHUNK_PAIRS = 4
-CHUNKS = PAIRS // CHUNK_PAIRS
-CHUNK_COLS = CHUNK_PAIRS * STEP_COLS
+LOAD_AHEAD = 4
 GROUPED_BUFS = 3
 
 FLOPS = 2 * BATCH * DIM * HID + 2 * BATCH * HID * (TAIL0 + 3 * DIM)
@@ -37,7 +35,7 @@ def tile_cn_pa_kernel(tc, x, cond, W1, b1, W2, b2, out):
     nc = tc.nc
     with ExitStack() as ctx:
         const = ctx.enter_context(tc.tile_pool(name="const", bufs=1))
-        raw_pool = ctx.enter_context(tc.tile_pool(name="raw", bufs=6))
+        raw_pool = ctx.enter_context(tc.tile_pool(name="raw", bufs=LOAD_AHEAD + 1))
         mx_pool = ctx.enter_context(tc.tile_pool(name="mx", bufs=3))
         work = ctx.enter_context(tc.tile_pool(name="work", bufs=3))
 
@@ -70,11 +68,11 @@ def tile_cn_pa_kernel(tc, x, cond, W1, b1, W2, b2, out):
 
         spread = const.tile([P, DL + 2], BF16)
         nc.gpsimd.memset(spread[:, DL : DL + 2], 0.0)
-        feats = DIM // CHUNKS
-        for g in range(CHUNKS):
+        feats = 16
+        for d0 in range(0, DIM, feats):
             nc.gpsimd.tensor_scalar(
-                out=spread[:, g * CHUNK_COLS : (g + 1) * CHUNK_COLS].rearrange("p (d l) -> p d l", l=LS),
-                in0=ident[:, g * feats : (g + 1) * feats].unsqueeze(2).to_broadcast([P, feats, LS]),
+                out=spread[:, d0 * LS : (d0 + feats) * LS].rearrange("p (d l) -> p d l", l=LS),
+                in0=ident[:, d0 : d0 + feats].unsqueeze(2).to_broadcast([P, feats, LS]),
                 scalar1=1.0,
                 scalar2=0.0,
                 op0=ALU.mult,
@@ -145,9 +143,11 @@ def tile_cn_pa_kernel(tc, x, cond, W1, b1, W2, b2, out):
 
         grouped_tiles = []
         for i in range(GROUPED_BUFS):
-            grouped = const.tile([P, SECTIONS, 2, P, PACK], BF16, name="grouped%d" % i, align_bytes=64)
+            grouped = const.tile([P, 2, 2, P, PACK], BF16, name="grouped%d" % i, align_bytes=64)
             nc.vector.memset(grouped[:, :, :, P - 16 : P, :], 0.0)
             grouped_tiles.append(grouped)
+        grouped_mat2 = const.tile([P, 2, P, PACK], BF16, align_bytes=64)
+        nc.vector.memset(grouped_mat2[:, :, P - 16 : P, :], 0.0)
 
         w2_by_p = W2.rearrange("(p j) c -> p j c", j=PACK)
 
@@ -159,41 +159,44 @@ def tile_cn_pa_kernel(tc, x, cond, W1, b1, W2, b2, out):
         tail_scales = const.tile([P, 3 * DIM], U8, align_bytes=64)
         tail = const.tile([P, HALVES, 3, DIM], F32)
 
-        raws = []
+        raw_of = []
 
-        def load_chunk(g):
-            raws.append([])
+        def load(n):
+            raw = raw_pool.tile([P, SECTIONS, PACK, STEP_COLS], BF16, name="raw")
             for s in range(SECTIONS):
-                raw = raw_pool.tile([P, PACK, CHUNK_COLS], BF16, name="raw")
-                col0 = s * DL + g * CHUNK_COLS
-                nc.sync.dma_start(out=raw[:], in_=w2_by_p[:, :, col0 : col0 + CHUNK_COLS])
-                raws[g].append(raw)
+                col0 = s * DL + n * STEP_COLS
+                nc.sync.dma_start(out=raw[:, s, :, :], in_=w2_by_p[:, :, col0 : col0 + STEP_COLS])
+            raw_of.append(raw)
 
         codes_of, scales_of, p_ps_of, x_e_ps_of, x_e_of = [], [], [], [], []
-        mat2_of, z1_of, m1m2_of, ez_of, num_of, den_of = [], [], [], [], [], []
+        mat2_of, z1_of, m1m2_of, ez_of, elu1_of, num_of, den_of = [], [], [], [], [], [], []
 
-        def regroup(n):
-            grouped = grouped_tiles[n % GROUPED_BUFS]
-            first = (n % CHUNK_PAIRS) * STEP_COLS
-            for s in range(SECTIONS):
-                src = raws[n // CHUNK_PAIRS][s][:, :, first : first + STEP_COLS].rearrange(
-                    "p j (t w) -> p t w j", w=PAIR_COLS
-                )
-                if s < 2:
-                    nc.scalar.copy(out=grouped[:, s, :, 0:PAIR_COLS, :], in_=src)
-                else:
-                    nc.vector.tensor_copy(out=grouped[:, s, :, 0:PAIR_COLS, :], in_=src)
+        def by_column(n, s):
+            return raw_of[n][:, s, :, :].rearrange("p j (t w) -> p t w j", w=PAIR_COLS)
+
+        def regroup_on_scalar(n):
+            for s in range(2):
+                nc.scalar.copy(out=grouped_tiles[n % GROUPED_BUFS][:, s, :, 0:PAIR_COLS, :], in_=by_column(n, s))
+
+        def regroup_on_gpsimd(n):
+            nc.gpsimd.tensor_scalar(
+                out=grouped_mat2[:, :, 0:PAIR_COLS, :], in0=by_column(n, 2),
+                scalar1=1.0, scalar2=0.0, op0=ALU.mult, op1=ALU.add,
+            )
 
         def quantise(n):
-            grouped = grouped_tiles[n % GROUPED_BUFS]
             codes = mx_pool.tile([P, SECTIONS, 2 * P], U32, name="codes", align_bytes=64)
             scales = mx_pool.tile([P, SECTIONS, 2 * P], U8, name="scales", align_bytes=64)
-            for s in range(SECTIONS):
-                nc.vector.quantize_mx(
-                    out=codes[:, s, :].bitcast(FP8X4),
-                    scales=scales[:, s, :],
-                    in_=grouped[:, s, :, :, :].rearrange("p t w j -> p (t w j)"),
-                )
+            nc.vector.quantize_mx(
+                out=codes[:, 2, :].bitcast(FP8X4),
+                scales=scales[:, 2, :],
+                in_=grouped_mat2[:].rearrange("p t w j -> p (t w j)"),
+            )
+            nc.vector.quantize_mx(
+                out=codes[:, 0:2, :].rearrange("p s w -> p (s w)").bitcast(FP8X4),
+                scales=scales[:, 0:2, :].rearrange("p s w -> p (s w)"),
+                in_=grouped_tiles[n % GROUPED_BUFS][:].rearrange("p s t w j -> p (s t w j)"),
+            )
             codes_of.append(codes)
             scales_of.append(scales)
 
@@ -242,41 +245,50 @@ def tile_cn_pa_kernel(tc, x, cond, W1, b1, W2, b2, out):
             z1 = work.tile([P, 2, BATCH], F32, name="z1")
             m1m2 = work.tile([P, 2, BATCH], F32, name="m1m2")
             p_ps = p_ps_of[n]
+            bias = [bias_t[:, :, 2 * n + u : 2 * n + u + 1] for u in range(2)]
             for u in range(2):
-                c = 2 * n + u
                 nc.vector.scalar_tensor_tensor(
-                    out=xm1[:, u, :], in0=p_ps[0][:, u, :], scalar=bias_t[:, 0, c : c + 1],
-                    in1=x_e_of[n][:, u, :], op0=ALU.add, op1=ALU.mult,
-                )
-                nc.vector.scalar_tensor_tensor(
-                    out=m1m2[:, u, :], in0=p_ps[0][:, u, :], scalar=bias_t[:, 0, c : c + 1],
+                    out=m1m2[:, u, :], in0=p_ps[0][:, u, :], scalar=bias[u][:, 0, :],
                     in1=mat2_of[n][:, u, :], op0=ALU.add, op1=ALU.mult,
                 )
+            for u in range(2):
                 nc.vector.scalar_tensor_tensor(
-                    out=z1[:, u, :], in0=p_ps[1][:, u, :], scalar=bias_t[:, 1, c : c + 1],
+                    out=xm1[:, u, :], in0=p_ps[0][:, u, :], scalar=bias[u][:, 0, :],
+                    in1=x_e_of[n][:, u, :], op0=ALU.add, op1=ALU.mult,
+                )
+            for u in range(2):
+                nc.vector.scalar_tensor_tensor(
+                    out=z1[:, u, :], in0=p_ps[1][:, u, :], scalar=bias[u][:, 1, :],
                     in1=xm1[:, u, :], op0=ALU.add, op1=ALU.add,
                 )
             z1_of.append(z1)
             m1m2_of.append(m1m2)
 
-        def functions(n):
-            ez = work.tile([P, 2, BATCH], F32, name="ez")
-            den_terms = work.tile([P, 2, BATCH], F32, name="den_terms")
-            nc.scalar.activation(out=ez[:], in_=z1_of[n][:], func=ACT.Exp, bias=minus_one[:], scale=1.0)
-            nc.scalar.activation(out=den_terms[:], in_=m1m2_of[n][:], func=ACT.Relu, scale=-1.0)
-            ez_of.append(ez)
-            den_of.append(den_terms)
+        def den_terms(n):
+            terms = work.tile([P, 2, BATCH], F32, name="den_terms")
+            nc.vector.tensor_scalar(
+                out=terms[:], in0=m1m2_of[n][:], scalar1=-1.0, scalar2=0.0, op0=ALU.mult, op1=ALU.max
+            )
+            den_of.append(terms)
 
-        def elu_terms(n):
+        def exponential(n):
+            ez = work.tile([P, 2, BATCH], F32, name="ez")
+            nc.scalar.activation(out=ez[:], in_=z1_of[n][:], func=ACT.Exp, bias=minus_one[:], scale=1.0)
+            ez_of.append(ez)
+
+        def elu_plus_one(n):
             elu1 = work.tile([P, 2, BATCH], F32, name="elu1")
-            num_terms = work.tile([P, 2, BATCH], F32, name="num_terms")
             nc.vector.scalar_tensor_tensor(
                 out=elu1[:], in0=ez_of[n][:], scalar=1.0, in1=z1_of[n][:], op0=ALU.min, op1=ALU.max
             )
+            elu1_of.append(elu1)
+
+        def num_terms(n):
+            terms = work.tile([P, 2, BATCH], F32, name="num_terms")
             nc.vector.scalar_tensor_tensor(
-                out=num_terms[:], in0=elu1[:], scalar=-1.0, in1=mat2_of[n][:], op0=ALU.add, op1=ALU.mult
+                out=terms[:], in0=elu1_of[n][:], scalar=-1.0, in1=mat2_of[n][:], op0=ALU.add, op1=ALU.mult
             )
-            num_of.append(num_terms)
+            num_of.append(terms)
 
         def add_up(n):
             for u in range(2):
@@ -296,7 +308,7 @@ def tile_cn_pa_kernel(tc, x, cond, W1, b1, W2, b2, out):
             if 0 <= n < PAIRS:
                 stage(n)
 
-        load_chunk(0)
+        load(0)
         nc.sync.dma_start(out=tail_raw[:], in_=w2_by_p[:, :, TAIL0 : TAIL0 + 3 * DIM])
         nc.vector.tensor_copy(out=tail_grouped[:], in_=tail_raw[:].rearrange("p j w -> p w j"))
         for i in range(3):
@@ -335,20 +347,23 @@ def tile_cn_pa_kernel(tc, x, cond, W1, b1, W2, b2, out):
         nc.vector.tensor_tensor(out=base[:], in0=exp_alpha[:], in1=x_f[:], op=ALU.mult)
         nc.vector.tensor_tensor(out=base[:], in0=base[:], in1=tail[:, :, 0, :], op=ALU.add)
 
-        load_chunk(1)
+        for n in range(1, LOAD_AHEAD):
+            load(n)
 
         with tc.manual_schedule():
             for step in range(PAIRS + 5):
-                run(functions, step - 4)
-                run(fetch, step - 3)
-                run(quantise, step - 1)
-                run(regroup, step)
-                if step % CHUNK_PAIRS == CHUNK_PAIRS - 1 and step // CHUNK_PAIRS + 2 < CHUNKS:
-                    load_chunk(step // CHUNK_PAIRS + 2)
-                run(elu_terms, step - 4)
-                run(products, step - 3)
+                run(load, step + LOAD_AHEAD)
                 run(multiply, step - 2)
                 run(add_up, step - 5)
+                run(regroup_on_scalar, step)
+                run(fetch, step - 2)
+                run(quantise, step - 1)
+                run(regroup_on_gpsimd, step)
+                run(products, step - 3)
+                run(exponential, step - 3)
+                run(elu_plus_one, step - 4)
+                run(den_terms, step - 3)
+                run(num_terms, step - 4)
 
         flat = "p h d -> p (h d)"
         divisor = const.tile([P, HALVES, DIM], F32)

@@ -25,6 +25,8 @@ PAIR_COLS = 2 * LS
 TILES = DIM // 2
 PAIRS = TILES // 2
 STEP_COLS = 2 * PAIR_COLS
+SPARE = P - PAIR_COLS
+RUN = 4
 LOAD_AHEAD = 4
 GROUPED_BUFS = 3
 
@@ -36,6 +38,7 @@ def tile_cn_pa_kernel(tc, x, cond, W1, b1, W2, b2, out):
     with ExitStack() as ctx:
         const = ctx.enter_context(tc.tile_pool(name="const", bufs=1))
         raw_pool = ctx.enter_context(tc.tile_pool(name="raw", bufs=LOAD_AHEAD + 1))
+        grouped_pool = ctx.enter_context(tc.tile_pool(name="grouped", bufs=GROUPED_BUFS))
         mx_pool = ctx.enter_context(tc.tile_pool(name="mx", bufs=3))
         work = ctx.enter_context(tc.tile_pool(name="work", bufs=3))
 
@@ -141,13 +144,7 @@ def tile_cn_pa_kernel(tc, x, cond, W1, b1, W2, b2, out):
         psum = ctx.enter_context(tc.psum_pool(name="psum", bufs=2))
         psum_one = ctx.enter_context(tc.psum_pool(name="psum_one", bufs=1))
 
-        grouped_tiles = []
-        for i in range(GROUPED_BUFS):
-            grouped = const.tile([P, 2, 2, P, PACK], BF16, name="grouped%d" % i, align_bytes=64)
-            nc.vector.memset(grouped[:, :, :, P - 16 : P, :], 0.0)
-            grouped_tiles.append(grouped)
         grouped_mat2 = const.tile([P, 2, P, PACK], BF16, align_bytes=64)
-        nc.vector.memset(grouped_mat2[:, :, P - 16 : P, :], 0.0)
 
         w2_by_p = W2.rearrange("(p j) c -> p j c", j=PACK)
 
@@ -162,27 +159,35 @@ def tile_cn_pa_kernel(tc, x, cond, W1, b1, W2, b2, out):
         raw_of = []
 
         def load(n):
-            raw = raw_pool.tile([P, SECTIONS, PACK, STEP_COLS], BF16, name="raw")
+            raw = raw_pool.tile([P, SECTIONS, PACK, 2 * P], BF16, name="raw")
+            width = STEP_COLS + SPARE
             for s in range(SECTIONS):
                 col0 = s * DL + n * STEP_COLS
-                nc.sync.dma_start(out=raw[:, s, :, :], in_=w2_by_p[:, :, col0 : col0 + STEP_COLS])
+                nc.sync.dma_start(out=raw[:, s, :, 0:width], in_=w2_by_p[:, :, col0 : col0 + width])
             raw_of.append(raw)
 
-        codes_of, scales_of, p_ps_of, x_e_ps_of, x_e_of = [], [], [], [], []
+        grouped_of, codes_of, scales_of, p_ps_of, x_e_ps_of, x_e_of = [], [], [], [], [], []
         mat2_of, z1_of, m1m2_of, ez_of, elu1_of, num_of, den_of = [], [], [], [], [], [], []
 
-        def by_column(n, s):
-            return raw_of[n][:, s, :, :].rearrange("p j (t w) -> p t w j", w=PAIR_COLS)
-
         def regroup_on_scalar(n):
+            grouped = grouped_pool.tile([P, 2, 2, P, PACK], BF16, name="grouped", align_bytes=64)
             for s in range(2):
-                nc.scalar.copy(out=grouped_tiles[n % GROUPED_BUFS][:, s, :, 0:PAIR_COLS, :], in_=by_column(n, s))
+                for t in range(2):
+                    nc.scalar.copy(
+                        out=grouped[:, s, t, :, :].rearrange("p (c i) j -> p c j i", i=RUN),
+                        in_=raw_of[n][:, s, :, t * PAIR_COLS : t * PAIR_COLS + P].rearrange(
+                            "p j (c i) -> p c j i", i=RUN
+                        ),
+                    )
+            grouped_of.append(grouped)
 
         def regroup_on_gpsimd(n):
-            nc.gpsimd.tensor_scalar(
-                out=grouped_mat2[:, :, 0:PAIR_COLS, :], in0=by_column(n, 2),
-                scalar1=1.0, scalar2=0.0, op0=ALU.mult, op1=ALU.add,
-            )
+            for t in range(2):
+                nc.gpsimd.tensor_scalar(
+                    out=grouped_mat2[:, t, :, :],
+                    in0=raw_of[n][:, 2, :, t * PAIR_COLS : t * PAIR_COLS + P].rearrange("p j w -> p w j"),
+                    scalar1=1.0, scalar2=0.0, op0=ALU.mult, op1=ALU.add,
+                )
 
         def quantise(n):
             codes = mx_pool.tile([P, SECTIONS, 2 * P], U32, name="codes", align_bytes=64)
@@ -195,7 +200,7 @@ def tile_cn_pa_kernel(tc, x, cond, W1, b1, W2, b2, out):
             nc.vector.quantize_mx(
                 out=codes[:, 0:2, :].rearrange("p s w -> p (s w)").bitcast(FP8X4),
                 scales=scales[:, 0:2, :].rearrange("p s w -> p (s w)"),
-                in_=grouped_tiles[n % GROUPED_BUFS][:].rearrange("p s t w j -> p (s t w j)"),
+                in_=grouped_of[n][:].rearrange("p s t w j -> p (s t w j)"),
             )
             codes_of.append(codes)
             scales_of.append(scales)

@@ -29,6 +29,7 @@ SPARE = P - PAIR_COLS
 RUN = 4
 LOAD_AHEAD = 4
 GROUPED_BUFS = 3
+FILL_UNITS = 3
 
 FLOPS = 2 * BATCH * DIM * HID + 2 * BATCH * HID * (TAIL0 + 3 * DIM)
 
@@ -172,8 +173,9 @@ def tile_cn_pa_kernel(tc, x, cond, W1, b1, W2, b2, out):
         def regroup_on_scalar(n):
             grouped = grouped_pool.tile([P, 2, 2, P, PACK], BF16, name="grouped", align_bytes=64)
             for s in range(2):
+                copy = nc.vector.tensor_copy if s == 1 and n < FILL_UNITS else nc.scalar.copy
                 for t in range(2):
-                    nc.scalar.copy(
+                    copy(
                         out=grouped[:, s, t, :, :].rearrange("p (c i) j -> p c j i", i=RUN),
                         in_=raw_of[n][:, s, :, t * PAIR_COLS : t * PAIR_COLS + P].rearrange(
                             "p j (c i) -> p c j i", i=RUN
@@ -193,44 +195,41 @@ def tile_cn_pa_kernel(tc, x, cond, W1, b1, W2, b2, out):
             codes = mx_pool.tile([P, SECTIONS, 2 * P], U32, name="codes", align_bytes=64)
             scales = mx_pool.tile([P, SECTIONS, 2 * P], U8, name="scales", align_bytes=64)
             nc.vector.quantize_mx(
-                out=codes[:, 2, :].bitcast(FP8X4),
-                scales=scales[:, 2, :],
-                in_=grouped_mat2[:].rearrange("p t w j -> p (t w j)"),
-            )
-            nc.vector.quantize_mx(
                 out=codes[:, 0:2, :].rearrange("p s w -> p (s w)").bitcast(FP8X4),
                 scales=scales[:, 0:2, :].rearrange("p s w -> p (s w)"),
                 in_=grouped_of[n][:].rearrange("p s t w j -> p (s t w j)"),
             )
+            nc.vector.quantize_mx(
+                out=codes[:, 2, :].bitcast(FP8X4),
+                scales=scales[:, 2, :],
+                in_=grouped_mat2[:].rearrange("p t w j -> p (t w j)"),
+            )
             codes_of.append(codes)
             scales_of.append(scales)
 
-        def multiply(n):
-            p_ps = [psum.tile([P, 2, BATCH], F32, name="p_ps%d" % s) for s in range(SECTIONS)]
-            for u in range(2):
-                cols = slice(u * P, (u + 1) * P)
-                for s in range(SECTIONS):
-                    nc.tensor.matmul_mx(
-                        out=p_ps[s][:, u, :],
-                        lhsT=codes_of[n][:, s, cols].bitcast(FP8X4),
-                        lhsT_scale=scales_of[n][:, s, cols],
-                        rhs=h_codes[:].bitcast(FP8X4),
-                        rhs_scale=h_scales[:],
-                        start=True,
-                        stop=True,
-                    )
-            x_e_ps = psum_one.tile([P, 2, BATCH], BF16, name="x_e_ps", tag="misc")
-            for u in range(2):
-                c = 2 * n + u
-                nc.tensor.matmul(
-                    out=x_e_ps[:, u, :],
-                    lhsT=spread[:, c * PAIR_COLS : c * PAIR_COLS + P],
-                    rhs=x_t[:],
+        def multiply(n, u):
+            if u == 0:
+                p_ps_of.append([psum.tile([P, 2, BATCH], F32, name="p_ps%d" % s) for s in range(SECTIONS)])
+                x_e_ps_of.append(psum_one.tile([P, 2, BATCH], BF16, name="x_e_ps", tag="misc"))
+            cols = slice(u * P, (u + 1) * P)
+            for s in range(SECTIONS):
+                nc.tensor.matmul_mx(
+                    out=p_ps_of[n][s][:, u, :],
+                    lhsT=codes_of[n][:, s, cols].bitcast(FP8X4),
+                    lhsT_scale=scales_of[n][:, s, cols],
+                    rhs=h_codes[:].bitcast(FP8X4),
+                    rhs_scale=h_scales[:],
                     start=True,
                     stop=True,
                 )
-            p_ps_of.append(p_ps)
-            x_e_ps_of.append(x_e_ps)
+            c = 2 * n + u
+            nc.tensor.matmul(
+                out=x_e_ps_of[n][:, u, :],
+                lhsT=spread[:, c * PAIR_COLS : c * PAIR_COLS + P],
+                rhs=x_t[:],
+                start=True,
+                stop=True,
+            )
 
         def fetch(n):
             mat2 = work.tile([P, 2, BATCH], F32, name="mat2")
@@ -295,23 +294,22 @@ def tile_cn_pa_kernel(tc, x, cond, W1, b1, W2, b2, out):
             )
             num_of.append(terms)
 
-        def add_up(n):
-            for u in range(2):
-                c = 2 * n + u
-                for h in range(HALVES):
-                    samples = slice(h * P, (h + 1) * P)
-                    for kind, terms in enumerate((num_of[n], den_of[n])):
-                        nc.tensor.matmul(
-                            out=sums[:, kind, h, 2 * c : 2 * c + 2],
-                            lhsT=terms[:, u, samples],
-                            rhs=pick[:],
-                            start=True,
-                            stop=True,
-                        )
+        def add_up(n, u):
+            c = 2 * n + u
+            for h in range(HALVES):
+                samples = slice(h * P, (h + 1) * P)
+                for kind, terms in enumerate((num_of[n], den_of[n])):
+                    nc.tensor.matmul(
+                        out=sums[:, kind, h, 2 * c : 2 * c + 2],
+                        lhsT=terms[:, u, samples],
+                        rhs=pick[:],
+                        start=True,
+                        stop=True,
+                    )
 
-        def run(stage, n):
+        def run(stage, n, *tile_of_unit):
             if 0 <= n < PAIRS:
-                stage(n)
+                stage(n, *tile_of_unit)
 
         load(0)
         nc.sync.dma_start(out=tail_raw[:], in_=w2_by_p[:, :, TAIL0 : TAIL0 + 3 * DIM])
@@ -358,8 +356,9 @@ def tile_cn_pa_kernel(tc, x, cond, W1, b1, W2, b2, out):
         with tc.manual_schedule():
             for step in range(PAIRS + 5):
                 run(load, step + LOAD_AHEAD)
-                run(multiply, step - 2)
-                run(add_up, step - 5)
+                for u in range(2):
+                    run(multiply, step - 2, u)
+                    run(add_up, step - 5, u)
                 run(regroup_on_scalar, step)
                 run(fetch, step - 2)
                 run(quantise, step - 1)

@@ -29,6 +29,7 @@ SPARE = P - PAIR_COLS
 RUN = 4
 LOAD_AHEAD = 4
 GROUPED_BUFS = 3
+X_CHUNK = 16
 FILL_UNITS = 3
 
 FLOPS = 2 * BATCH * DIM * HID + 2 * BATCH * HID * (TAIL0 + 3 * DIM)
@@ -53,10 +54,10 @@ def tile_cn_pa_kernel(tc, x, cond, W1, b1, W2, b2, out):
         nc.vector.memset(b2_rows_a[:], 0.0)
         nc.vector.memset(b2_rows_b[:], 0.0)
         with nc.allow_non_contiguous_dma(reason="small inputs, loaded once"):
+            nc.scalar.dma_start(out=x_sb[:], in_=x.rearrange("(h p) d -> p h d", p=P))
             nc.scalar.dma_start(out=cond_sb[:], in_=cond.rearrange("(h p) d -> p h d", p=P))
             nc.scalar.dma_start(out=w1_sb[:], in_=W1)
             nc.scalar.dma_start(out=b1_sb[:], in_=b1.rearrange("(p j) -> p j", j=PACK))
-            nc.scalar.dma_start(out=x_sb[:], in_=x.rearrange("(h p) d -> p h d", p=P))
             nc.scalar.dma_start(
                 out=b2_rows_a[:, 0:PAIR_COLS],
                 in_=b2[0 : P * PAIR_COLS].rearrange("(r m) -> r m", m=PAIR_COLS),
@@ -70,18 +71,16 @@ def tile_cn_pa_kernel(tc, x, cond, W1, b1, W2, b2, out):
         ident = const.tile([P, P], BF16)
         make_identity(nc, ident[:])
 
-        spread = const.tile([P, DL + 2], BF16)
-        nc.gpsimd.memset(spread[:, DL : DL + 2], 0.0)
-        feats = 16
-        for d0 in range(0, DIM, feats):
-            nc.gpsimd.tensor_scalar(
-                out=spread[:, d0 * LS : (d0 + feats) * LS].rearrange("p (d l) -> p d l", l=LS),
-                in0=ident[:, d0 : d0 + feats].unsqueeze(2).to_broadcast([P, feats, LS]),
-                scalar1=1.0,
-                scalar2=0.0,
-                op0=ALU.mult,
-                op1=ALU.add,
-            )
+        pick_t = const.tile([P, P], BF16)
+        nc.gpsimd.memset(pick_t[:, PAIR_COLS:P], 0.0)
+        nc.gpsimd.tensor_scalar(
+            out=pick_t[:, 0:PAIR_COLS].rearrange("p (d l) -> p d l", l=LS),
+            in0=ident[:, 0:2].unsqueeze(2).to_broadcast([P, 2, LS]),
+            scalar1=1.0,
+            scalar2=0.0,
+            op0=ALU.mult,
+            op1=ALU.add,
+        )
 
         x_t = const.tile([P, BATCH], BF16)
         cond_t = const.tile([P, BATCH], BF16)
@@ -101,11 +100,12 @@ def tile_cn_pa_kernel(tc, x, cond, W1, b1, W2, b2, out):
             cond_t_ps = psum_start.tile([P, BATCH], BF16)
             x_t_ps = psum_start.tile([P, BATCH], BF16)
             for h in range(HALVES):
-                nc.tensor.transpose(cond_t_ps[:, h * P : (h + 1) * P], cond_sb[:, h, :], ident[:])
-            nc.vector.tensor_copy(out=cond_t[:], in_=cond_t_ps[:])
-            for h in range(HALVES):
                 nc.tensor.transpose(x_t_ps[:, h * P : (h + 1) * P], x_sb[:, h, :], ident[:])
             nc.vector.tensor_copy(out=x_t[:], in_=x_t_ps[:])
+            nc.sync.dma_start(out=out[0:DIM, :], in_=x_t[:].bitcast(F32))
+            for h in range(HALVES):
+                nc.tensor.transpose(cond_t_ps[:, h * P : (h + 1) * P], cond_sb[:, h, :], ident[:])
+            nc.vector.tensor_copy(out=cond_t[:], in_=cond_t_ps[:])
 
             w1_by_j = w1_sb[:].rearrange("k (p j) -> k j p", j=PACK)
             h_ps = [
@@ -139,7 +139,7 @@ def tile_cn_pa_kernel(tc, x, cond, W1, b1, W2, b2, out):
             nc.vector.tensor_scalar_add(out=bias_t[:, 1, :], in0=bias_t[:, 1, :], scalar1=1.0)
 
             pick_ps = psum_start.tile([P, P], BF16)
-            nc.tensor.transpose(pick_ps[:], spread[:, 0:P], ident[:])
+            nc.tensor.transpose(pick_ps[:], pick_t[:], ident[:])
             nc.vector.tensor_copy(out=pick[:], in_=pick_ps[:, 0:2])
 
         psum = ctx.enter_context(tc.psum_pool(name="psum", bufs=2))
@@ -157,6 +157,14 @@ def tile_cn_pa_kernel(tc, x, cond, W1, b1, W2, b2, out):
         tail_scales = const.tile([P, 3 * DIM], U8, align_bytes=64)
         tail = const.tile([P, HALVES, 3, DIM], F32)
 
+        x_e = const.tile([P, TILES, BATCH // 2], F32)
+
+        def load_x(chunk):
+            tiles = slice(chunk * X_CHUNK, (chunk + 1) * X_CHUNK)
+            for e, parts in enumerate((slice(0, LS), slice(LS, P))):
+                rows = out[2 * tiles.start + e : 2 * tiles.stop : 2, :]
+                nc.sync.dma_start(out=x_e[parts, tiles, :], in_=rows.partition_broadcast(parts.stop - parts.start))
+
         raw_of = []
 
         def load(n):
@@ -167,7 +175,7 @@ def tile_cn_pa_kernel(tc, x, cond, W1, b1, W2, b2, out):
                 nc.sync.dma_start(out=raw[:, s, :, 0:width], in_=w2_by_p[:, :, col0 : col0 + width])
             raw_of.append(raw)
 
-        grouped_of, codes_of, scales_of, p_ps_of, x_e_ps_of, x_e_of = [], [], [], [], [], []
+        grouped_of, codes_of, scales_of, p_ps_of = [], [], [], []
         mat2_of, z1_of, m1m2_of, ez_of, elu1_of, num_of, den_of = [], [], [], [], [], [], []
 
         def regroup_on_scalar(n):
@@ -210,7 +218,6 @@ def tile_cn_pa_kernel(tc, x, cond, W1, b1, W2, b2, out):
         def multiply(n, u):
             if u == 0:
                 p_ps_of.append([psum.tile([P, 2, BATCH], F32, name="p_ps%d" % s) for s in range(SECTIONS)])
-                x_e_ps_of.append(psum_one.tile([P, 2, BATCH], BF16, name="x_e_ps", tag="misc"))
             cols = slice(u * P, (u + 1) * P)
             for s in range(SECTIONS):
                 nc.tensor.matmul_mx(
@@ -222,27 +229,16 @@ def tile_cn_pa_kernel(tc, x, cond, W1, b1, W2, b2, out):
                     start=True,
                     stop=True,
                 )
-            c = 2 * n + u
-            nc.tensor.matmul(
-                out=x_e_ps_of[n][:, u, :],
-                lhsT=spread[:, c * PAIR_COLS : c * PAIR_COLS + P],
-                rhs=x_t[:],
-                start=True,
-                stop=True,
-            )
 
         def fetch(n):
             mat2 = work.tile([P, 2, BATCH], F32, name="mat2")
-            x_e = work.tile([P, 2, BATCH], BF16, name="x_e")
             for u in range(2):
                 c = 2 * n + u
                 nc.scalar.activation(
                     out=mat2[:, u, :], in_=p_ps_of[n][2][:, u, :], func=ACT.Identity,
                     bias=bias_t[:, 2, c : c + 1], scale=1.0,
                 )
-            nc.scalar.copy(out=x_e[:], in_=x_e_ps_of[n][:])
             mat2_of.append(mat2)
-            x_e_of.append(x_e)
 
         def products(n):
             xm1 = work.tile([P, 2, BATCH], F32, name="xm1")
@@ -258,7 +254,7 @@ def tile_cn_pa_kernel(tc, x, cond, W1, b1, W2, b2, out):
             for u in range(2):
                 nc.vector.scalar_tensor_tensor(
                     out=xm1[:, u, :], in0=p_ps[0][:, u, :], scalar=bias[u][:, 0, :],
-                    in1=x_e_of[n][:, u, :], op0=ALU.add, op1=ALU.mult,
+                    in1=x_e[:, 2 * n + u, :].bitcast(BF16), op0=ALU.add, op1=ALU.mult,
                 )
             for u in range(2):
                 nc.vector.scalar_tensor_tensor(
@@ -356,6 +352,10 @@ def tile_cn_pa_kernel(tc, x, cond, W1, b1, W2, b2, out):
         with tc.manual_schedule():
             for step in range(PAIRS + 5):
                 run(load, step + LOAD_AHEAD)
+                if (step + 1) % (X_CHUNK // 2) == 0 or step == 0:
+                    chunk = (step + 1) // (X_CHUNK // 2)
+                    if chunk < TILES // X_CHUNK:
+                        load_x(chunk)
                 for u in range(2):
                     run(multiply, step - 2, u)
                     run(add_up, step - 5, u)

@@ -29,6 +29,7 @@ SPARE = P - PAIR_COLS
 RUN = 4
 LOAD_AHEAD = 4
 GROUPED_BUFS = 3
+WIDE = 64
 X_CHUNK = 16
 FILL_UNITS = 3
 
@@ -85,7 +86,7 @@ def tile_cn_pa_kernel(tc, x, cond, W1, b1, W2, b2, out):
         x_t = const.tile([P, BATCH], BF16)
         cond_t = const.tile([P, BATCH], BF16)
         bias_t = const.tile([P, SECTIONS, TILES], F32)
-        pick = const.tile([P, 2], F32)
+        pick = const.tile([P, WIDE], F32)
         b1_f = const.tile([P, PACK], F32)
         x_f = const.tile([P, HALVES, DIM], F32)
         h_grouped = const.tile([P, BATCH, PACK], BF16, align_bytes=64)
@@ -140,7 +141,7 @@ def tile_cn_pa_kernel(tc, x, cond, W1, b1, W2, b2, out):
 
             pick_ps = psum_start.tile([P, P], BF16)
             nc.tensor.transpose(pick_ps[:], pick_t[:], ident[:])
-            nc.vector.tensor_copy(out=pick[:], in_=pick_ps[:, 0:2])
+            nc.vector.tensor_copy(out=pick[:], in_=pick_ps[:, 0:WIDE])
 
         psum = ctx.enter_context(tc.psum_pool(name="psum", bufs=2))
         psum_one = ctx.enter_context(tc.psum_pool(name="psum_one", bufs=1))
@@ -149,7 +150,10 @@ def tile_cn_pa_kernel(tc, x, cond, W1, b1, W2, b2, out):
 
         w2_by_p = W2.rearrange("(p j) c -> p j c", j=PACK)
 
-        sums = psum_one.tile([P, 2, HALVES, DIM], F32)
+        sums = [
+            psum_one.tile([P, HALVES, DIM + WIDE - 2], F32, name="sums_num"),
+            psum_one.tile([P, HALVES, DIM + WIDE - 2], F32, name="sums_den"),
+        ]
 
         tail_raw = const.tile([P, PACK, 3 * DIM], BF16)
         tail_grouped = const.tile([P, 3 * DIM, PACK], BF16, align_bytes=64)
@@ -296,7 +300,7 @@ def tile_cn_pa_kernel(tc, x, cond, W1, b1, W2, b2, out):
                 samples = slice(h * P, (h + 1) * P)
                 for kind, terms in enumerate((num_of[n], den_of[n])):
                     nc.tensor.matmul(
-                        out=sums[:, kind, h, 2 * c : 2 * c + 2],
+                        out=sums[kind][:, h, 2 * c : 2 * c + WIDE],
                         lhsT=terms[:, u, samples],
                         rhs=pick[:],
                         start=True,
@@ -319,7 +323,7 @@ def tile_cn_pa_kernel(tc, x, cond, W1, b1, W2, b2, out):
             )
         for h in range(HALVES):
             samples = slice(h * P, (h + 1) * P)
-            tail_ps = psum_one.tile([P, 3, DIM], F32, name="tail_ps", tag="misc")
+            tail_ps = psum.tile([P, 3, DIM], F32, name="tail_ps", tag="p_ps0")
             for i in range(3):
                 cols = slice(i * DIM, (i + 1) * DIM)
                 nc.tensor.matmul_mx(
@@ -369,21 +373,15 @@ def tile_cn_pa_kernel(tc, x, cond, W1, b1, W2, b2, out):
                 run(den_terms, step - 3)
                 run(num_terms, step - 4)
 
-        flat = "p h d -> p (h d)"
         divisor = const.tile([P, HALVES, DIM], F32)
         result = const.tile([P, HALVES, DIM], F32)
         nc.vector.scalar_tensor_tensor(
-            out=divisor[:].rearrange(flat), in0=sums[:, 1, :, :].rearrange(flat), scalar=1.0,
-            in1=gate_den[:].rearrange(flat), op0=ALU.add, op1=ALU.mult,
+            out=divisor[:], in0=sums[1][:, :, 0:DIM], scalar=1.0, in1=gate_den[:], op0=ALU.add, op1=ALU.mult,
         )
         nc.vector.reciprocal(out=divisor[:], in_=divisor[:])
-        nc.vector.tensor_tensor(
-            out=result[:].rearrange(flat), in0=sums[:, 0, :, :].rearrange(flat),
-            in1=divisor[:].rearrange(flat), op=ALU.mult,
-        )
+        nc.vector.tensor_tensor(out=result[:], in0=sums[0][:, :, 0:DIM], in1=divisor[:], op=ALU.mult)
         nc.vector.scalar_tensor_tensor(
-            out=result[:].rearrange(flat), in0=result[:].rearrange(flat), scalar=0.8,
-            in1=exp_alpha[:].rearrange(flat), op0=ALU.mult, op1=ALU.mult,
+            out=result[:], in0=result[:], scalar=0.8, in1=exp_alpha[:], op0=ALU.mult, op1=ALU.mult
         )
         nc.vector.tensor_tensor(out=result[:], in0=result[:], in1=base[:], op=ALU.add)
         nc.sync.dma_start(out=out.rearrange("(h p) d -> p h d", p=P), in_=result[:])

@@ -270,9 +270,7 @@ def tile_cn_pa_kernel(tc, x, cond, W1, b1, W2, b2, out):
 
         def den_terms(n):
             terms = work.tile([P, 2, BATCH], F32, name="den_terms")
-            nc.vector.tensor_scalar(
-                out=terms[:], in0=m1m2_of[n][:], scalar1=-1.0, scalar2=0.0, op0=ALU.mult, op1=ALU.max
-            )
+            nc.scalar.activation(out=terms[:], in_=m1m2_of[n][:], func=ACT.Relu, scale=-1.0)
             den_of.append(terms)
 
         def exponential(n):
@@ -365,12 +363,12 @@ def tile_cn_pa_kernel(tc, x, cond, W1, b1, W2, b2, out):
                     run(add_up, step - 5, u)
                 run(regroup_on_scalar, step)
                 run(fetch, step - 2)
+                run(elu_plus_one, step - 4)
                 run(quantise, step - 1)
                 run(regroup_on_gpsimd, step)
                 run(products, step - 3)
-                run(exponential, step - 3)
-                run(elu_plus_one, step - 4)
                 run(den_terms, step - 3)
+                run(exponential, step - 3)
                 run(num_terms, step - 4)
 
         divisor = const.tile([P, HALVES, DIM], F32)

@@ -203,7 +203,7 @@ def tile_cn_pa_kernel(tc, x, cond, W1, b1, W2, b2, out):
                     scalar1=1.0, scalar2=0.0, op0=ALU.mult, op1=ALU.add,
                 )
 
-        def quantise(n):
+        def quantise_mat1_bias1(n):
             codes = mx_pool.tile([P, SECTIONS, 2 * P], U32, name="codes", align_bytes=64)
             scales = mx_pool.tile([P, SECTIONS, 2 * P], U8, name="scales", align_bytes=64)
             nc.vector.quantize_mx(
@@ -211,13 +211,15 @@ def tile_cn_pa_kernel(tc, x, cond, W1, b1, W2, b2, out):
                 scales=scales[:, 0:2, :].rearrange("p s w -> p (s w)"),
                 in_=grouped_of[n][:].rearrange("p s t w j -> p (s t w j)"),
             )
-            nc.vector.quantize_mx(
-                out=codes[:, 2, :].bitcast(FP8X4),
-                scales=scales[:, 2, :],
-                in_=grouped_mat2[:].rearrange("p t w j -> p (t w j)"),
-            )
             codes_of.append(codes)
             scales_of.append(scales)
+
+        def quantise_mat2(n):
+            nc.vector.quantize_mx(
+                out=codes_of[n][:, 2, :].bitcast(FP8X4),
+                scales=scales_of[n][:, 2, :],
+                in_=grouped_mat2[:].rearrange("p t w j -> p (t w j)"),
+            )
 
         def multiply(n, u):
             if u == 0:
@@ -235,7 +237,7 @@ def tile_cn_pa_kernel(tc, x, cond, W1, b1, W2, b2, out):
                 )
 
         def fetch(n):
-            mat2 = work.tile([P, 2, BATCH], F32, name="mat2")
+            mat2 = work.tile([P, 2, BATCH], F32, name="mat2", bufs=5)
             for u in range(2):
                 c = 2 * n + u
                 nc.scalar.activation(
@@ -269,7 +271,7 @@ def tile_cn_pa_kernel(tc, x, cond, W1, b1, W2, b2, out):
             m1m2_of.append(m1m2)
 
         def den_terms(n):
-            terms = work.tile([P, 2, BATCH], F32, name="den_terms")
+            terms = work.tile([P, 2, BATCH], F32, name="den_terms", bufs=4)
             nc.scalar.activation(out=terms[:], in_=m1m2_of[n][:], func=ACT.Relu, scale=-1.0)
             den_of.append(terms)
 
@@ -352,7 +354,7 @@ def tile_cn_pa_kernel(tc, x, cond, W1, b1, W2, b2, out):
             load(n)
 
         with tc.manual_schedule():
-            for step in range(PAIRS + 5):
+            for step in range(PAIRS + 8):
                 run(load, step + LOAD_AHEAD)
                 if (step + 1) % (X_CHUNK // 2) == 0 or step == 0:
                     chunk = (step + 1) // (X_CHUNK // 2)
@@ -360,16 +362,17 @@ def tile_cn_pa_kernel(tc, x, cond, W1, b1, W2, b2, out):
                         load_x(chunk)
                 for u in range(2):
                     run(multiply, step - 2, u)
-                    run(add_up, step - 5, u)
+                    run(add_up, step - 7, u)
                 run(regroup_on_scalar, step)
                 run(fetch, step - 2)
-                run(elu_plus_one, step - 4)
-                run(quantise, step - 1)
+                run(den_terms, step - 4)
+                run(exponential, step - 4)
+                run(quantise_mat1_bias1, step - 1)
+                run(num_terms, step - 6)
+                run(quantise_mat2, step - 1)
                 run(regroup_on_gpsimd, step)
                 run(products, step - 3)
-                run(den_terms, step - 3)
-                run(exponential, step - 3)
-                run(num_terms, step - 4)
+                run(elu_plus_one, step - 5)
 
         divisor = const.tile([P, HALVES, DIM], F32)
         result = const.tile([P, HALVES, DIM], F32)

@@ -271,7 +271,7 @@ def tile_cn_pa_kernel(tc, x, cond, W1, b1, W2, b2, out):
             m1m2_of.append(m1m2)
 
         def den_terms(n):
-            terms = work.tile([P, 2, BATCH], F32, name="den_terms", bufs=4)
+            terms = work.tile([P, 2, BATCH], F32, name="den_terms")
             nc.scalar.activation(out=terms[:], in_=m1m2_of[n][:], func=ACT.Relu, scale=-1.0)
             den_of.append(terms)
 
@@ -294,18 +294,17 @@ def tile_cn_pa_kernel(tc, x, cond, W1, b1, W2, b2, out):
             )
             num_of.append(terms)
 
-        def add_up(n, u):
+        def add_up(n, u, kind):
             c = 2 * n + u
+            terms = (num_of, den_of)[kind][n]
             for h in range(HALVES):
-                samples = slice(h * P, (h + 1) * P)
-                for kind, terms in enumerate((num_of[n], den_of[n])):
-                    nc.tensor.matmul(
-                        out=sums[kind][:, h, 2 * c : 2 * c + WIDE],
-                        lhsT=terms[:, u, samples],
-                        rhs=pick[:],
-                        start=True,
-                        stop=True,
-                    )
+                nc.tensor.matmul(
+                    out=sums[kind][:, h, 2 * c : 2 * c + WIDE],
+                    lhsT=terms[:, u, h * P : (h + 1) * P],
+                    rhs=pick[:],
+                    start=True,
+                    stop=True,
+                )
 
         def run(stage, n, *tile_of_unit):
             if 0 <= n < PAIRS:
@@ -362,7 +361,8 @@ def tile_cn_pa_kernel(tc, x, cond, W1, b1, W2, b2, out):
                         load_x(chunk)
                 for u in range(2):
                     run(multiply, step - 2, u)
-                    run(add_up, step - 7, u)
+                    run(add_up, step - 5, u, 1)
+                    run(add_up, step - 7, u, 0)
                 run(regroup_on_scalar, step)
                 run(fetch, step - 2)
                 run(den_terms, step - 4)

@@ -341,13 +341,20 @@ def tile_cn_pa_kernel(tc, x, cond, W1, b1, W2, b2, out):
                 op=ALU.add,
             )
         exp_alpha = const.tile([P, HALVES, DIM], F32)
+        exp_minus_alpha = const.tile([P, HALVES, DIM], F32)
         gate_den = const.tile([P, HALVES, DIM], F32)
         base = const.tile([P, HALVES, DIM], F32)
         nc.scalar.activation(out=exp_alpha[:], in_=tail[:, :, 2, :], func=ACT.Exp, scale=0.1)
+        nc.scalar.activation(out=exp_minus_alpha[:], in_=tail[:, :, 2, :], func=ACT.Exp, scale=-0.1)
         nc.scalar.activation(out=gate_den[:], in_=tail[:, :, 1, :], func=ACT.Exp, scale=-0.1)
-        nc.vector.tensor_scalar_add(out=gate_den[:], in0=gate_den[:], scalar1=1.0)
         nc.vector.tensor_tensor(out=base[:], in0=exp_alpha[:], in1=x_f[:], op=ALU.mult)
+        nc.vector.scalar_tensor_tensor(
+            out=gate_den[:], in0=gate_den[:], scalar=1.0, in1=exp_minus_alpha[:], op0=ALU.add, op1=ALU.mult
+        )
         nc.vector.tensor_tensor(out=base[:], in0=base[:], in1=tail[:, :, 0, :], op=ALU.add)
+        nc.vector.tensor_scalar_mul(out=gate_den[:], in0=gate_den[:], scalar1=1.25)
+        divisor = const.tile([P, HALVES, DIM], F32)
+        result = const.tile([P, HALVES, DIM], F32)
 
         for n in range(1, LOAD_AHEAD):
             load(n)
@@ -361,6 +368,7 @@ def tile_cn_pa_kernel(tc, x, cond, W1, b1, W2, b2, out):
                         load_x(chunk)
                 for u in range(2):
                     run(multiply, step - 2, u)
+                for u in range(2):
                     run(add_up, step - 5, u, 1)
                     run(add_up, step - 7, u, 0)
                 run(regroup_on_scalar, step)
@@ -368,21 +376,18 @@ def tile_cn_pa_kernel(tc, x, cond, W1, b1, W2, b2, out):
                 run(den_terms, step - 4)
                 run(exponential, step - 4)
                 run(quantise_mat1_bias1, step - 1)
-                run(num_terms, step - 6)
                 run(quantise_mat2, step - 1)
                 run(regroup_on_gpsimd, step)
                 run(products, step - 3)
+                run(num_terms, step - 6)
                 run(elu_plus_one, step - 5)
+                if step == PAIRS - 1 + 6:
+                    nc.vector.scalar_tensor_tensor(
+                        out=divisor[:], in0=sums[1][:, :, 0:DIM], scalar=1.0, in1=gate_den[:],
+                        op0=ALU.add, op1=ALU.mult,
+                    )
+                    nc.vector.reciprocal(out=divisor[:], in_=divisor[:])
 
-        divisor = const.tile([P, HALVES, DIM], F32)
-        result = const.tile([P, HALVES, DIM], F32)
-        nc.vector.scalar_tensor_tensor(
-            out=divisor[:], in0=sums[1][:, :, 0:DIM], scalar=1.0, in1=gate_den[:], op0=ALU.add, op1=ALU.mult,
-        )
-        nc.vector.reciprocal(out=divisor[:], in_=divisor[:])
         nc.vector.tensor_tensor(out=result[:], in0=sums[0][:, :, 0:DIM], in1=divisor[:], op=ALU.mult)
-        nc.vector.scalar_tensor_tensor(
-            out=result[:], in0=result[:], scalar=0.8, in1=exp_alpha[:], op0=ALU.mult, op1=ALU.mult
-        )
         nc.vector.tensor_tensor(out=result[:], in0=result[:], in1=base[:], op=ALU.add)
         nc.sync.dma_start(out=out.rearrange("(h p) d -> p h d", p=P), in_=result[:])

@@ -30,6 +30,7 @@ RUN = 4
 LOAD_AHEAD = 4
 GROUPED_BUFS = 3
 WIDE = 64
+WIDE_BESIDE_MX = 48
 X_CHUNK = 16
 FILL_UNITS = 3
 
@@ -294,14 +295,14 @@ def tile_cn_pa_kernel(tc, x, cond, W1, b1, W2, b2, out):
             )
             num_of.append(terms)
 
-        def add_up(n, u, kind):
+        def add_up(n, u, kind, wide):
             c = 2 * n + u
             terms = (num_of, den_of)[kind][n]
             for h in range(HALVES):
                 nc.tensor.matmul(
-                    out=sums[kind][:, h, 2 * c : 2 * c + WIDE],
+                    out=sums[kind][:, h, 2 * c : 2 * c + wide],
                     lhsT=terms[:, u, h * P : (h + 1) * P],
-                    rhs=pick[:],
+                    rhs=pick[:, 0:wide],
                     start=True,
                     stop=True,
                 )
@@ -368,9 +369,10 @@ def tile_cn_pa_kernel(tc, x, cond, W1, b1, W2, b2, out):
                         load_x(chunk)
                 for u in range(2):
                     run(multiply, step - 2, u)
+                wide = WIDE_BESIDE_MX if step - 2 < PAIRS else WIDE
                 for u in range(2):
-                    run(add_up, step - 5, u, 1)
-                    run(add_up, step - 7, u, 0)
+                    run(add_up, step - 5, u, 1, wide)
+                    run(add_up, step - 7, u, 0, wide)
                 run(regroup_on_scalar, step)
                 run(fetch, step - 2)
                 run(den_terms, step - 4)

@@ -148,6 +148,7 @@ def tile_cn_pa_kernel(tc, x, cond, W1, b1, W2, b2, out):
         psum_one = ctx.enter_context(tc.psum_pool(name="psum_one", bufs=1))
 
         grouped_mat2 = const.tile([P, 2, P, PACK], BF16, align_bytes=64)
+        nc.gpsimd.memset(grouped_mat2[:, :, PAIR_COLS:P, :], 0.0)
 
         w2_by_p = W2.rearrange("(p j) c -> p j c", j=PACK)
 
@@ -197,12 +198,11 @@ def tile_cn_pa_kernel(tc, x, cond, W1, b1, W2, b2, out):
             grouped_of.append(grouped)
 
         def regroup_on_gpsimd(n):
-            for t in range(2):
-                nc.gpsimd.tensor_scalar(
-                    out=grouped_mat2[:, t, :, :],
-                    in0=raw_of[n][:, 2, :, t * PAIR_COLS : t * PAIR_COLS + P].rearrange("p j w -> p w j"),
-                    scalar1=1.0, scalar2=0.0, op0=ALU.mult, op1=ALU.add,
-                )
+            nc.gpsimd.tensor_scalar(
+                out=grouped_mat2[:, :, 0:PAIR_COLS, :],
+                in0=raw_of[n][:, 2, :, 0:STEP_COLS].rearrange("p j (t w) -> p t w j", t=2),
+                scalar1=1.0, scalar2=0.0, op0=ALU.mult, op1=ALU.add,
+            )
 
         def quantise_mat1_bias1(n):
             codes = mx_pool.tile([P, SECTIONS, 2 * P], U32, name="codes", align_bytes=64)

@@ -31,7 +31,9 @@ LOAD_AHEAD = 4
 GROUPED_BUFS = 3
 WIDE = 64
 WIDE_BESIDE_MX = 48
-X_CHUNK = 16
+X_CHUNK = 8
+TAIL_STEP = 12
+EARLY_STEPS = 6
 FILL_UNITS = 3
 
 FLOPS = 2 * BATCH * DIM * HID + 2 * BATCH * HID * (TAIL0 + 3 * DIM)
@@ -45,6 +47,7 @@ def tile_cn_pa_kernel(tc, x, cond, W1, b1, W2, b2, out):
         grouped_pool = ctx.enter_context(tc.tile_pool(name="grouped", bufs=GROUPED_BUFS))
         mx_pool = ctx.enter_context(tc.tile_pool(name="mx", bufs=3))
         work = ctx.enter_context(tc.tile_pool(name="work", bufs=3))
+        ctx.enter_context(tc.manual_schedule())
 
         x_sb = const.tile([P, HALVES, DIM], BF16)
         cond_sb = const.tile([P, HALVES, DIM], BF16)
@@ -53,37 +56,8 @@ def tile_cn_pa_kernel(tc, x, cond, W1, b1, W2, b2, out):
         b2_rows_a = const.tile([P, P], BF16)
         b2_rows_b = const.tile([P, P], BF16)
         b2_tail = const.tile([P, 3 * DIM], BF16)
-        nc.vector.memset(b2_rows_a[:], 0.0)
-        nc.vector.memset(b2_rows_b[:], 0.0)
-        with nc.allow_non_contiguous_dma(reason="small inputs, loaded once"):
-            nc.scalar.dma_start(out=x_sb[:], in_=x.rearrange("(h p) d -> p h d", p=P))
-            nc.scalar.dma_start(out=cond_sb[:], in_=cond.rearrange("(h p) d -> p h d", p=P))
-            nc.scalar.dma_start(out=w1_sb[:], in_=W1)
-            nc.scalar.dma_start(out=b1_sb[:], in_=b1.rearrange("(p j) -> p j", j=PACK))
-            nc.scalar.dma_start(
-                out=b2_rows_a[:, 0:PAIR_COLS],
-                in_=b2[0 : P * PAIR_COLS].rearrange("(r m) -> r m", m=PAIR_COLS),
-            )
-            nc.scalar.dma_start(
-                out=b2_rows_b[0:TILES, 0:PAIR_COLS],
-                in_=b2[P * PAIR_COLS : TAIL0].rearrange("(r m) -> r m", m=PAIR_COLS),
-            )
-            nc.scalar.dma_start(out=b2_tail[:], in_=b2[TAIL0 : TAIL0 + 3 * DIM].partition_broadcast(P))
-
         ident = const.tile([P, P], BF16)
-        make_identity(nc, ident[:])
-
         pick_t = const.tile([P, P], BF16)
-        nc.gpsimd.memset(pick_t[:, PAIR_COLS:P], 0.0)
-        nc.gpsimd.tensor_scalar(
-            out=pick_t[:, 0:PAIR_COLS].rearrange("p (d l) -> p d l", l=LS),
-            in0=ident[:, 0:2].unsqueeze(2).to_broadcast([P, 2, LS]),
-            scalar1=1.0,
-            scalar2=0.0,
-            op0=ALU.mult,
-            op1=ALU.add,
-        )
-
         x_t = const.tile([P, BATCH], BF16)
         cond_t = const.tile([P, BATCH], BF16)
         bias_t = const.tile([P, SECTIONS, TILES], F32)
@@ -94,74 +68,23 @@ def tile_cn_pa_kernel(tc, x, cond, W1, b1, W2, b2, out):
         h_codes = const.tile([P, BATCH], U32, align_bytes=64)
         h_scales = const.tile([P, BATCH], U8, align_bytes=64)
         minus_one = const.tile([P, 1], F32)
-        nc.vector.memset(minus_one[:], -1.0)
-        nc.vector.tensor_copy(out=b1_f[:], in_=b1_sb[:])
-        nc.vector.tensor_copy(out=x_f[:], in_=x_sb[:])
-
-        with tc.psum_pool(name="psum_start", bufs=1) as psum_start:
-            cond_t_ps = psum_start.tile([P, BATCH], BF16)
-            x_t_ps = psum_start.tile([P, BATCH], BF16)
-            for h in range(HALVES):
-                nc.tensor.transpose(x_t_ps[:, h * P : (h + 1) * P], x_sb[:, h, :], ident[:])
-            nc.vector.tensor_copy(out=x_t[:], in_=x_t_ps[:])
-            nc.sync.dma_start(out=out[0:DIM, :], in_=x_t[:].bitcast(F32))
-            for h in range(HALVES):
-                nc.tensor.transpose(cond_t_ps[:, h * P : (h + 1) * P], cond_sb[:, h, :], ident[:])
-            nc.vector.tensor_copy(out=cond_t[:], in_=cond_t_ps[:])
-
-            w1_by_j = w1_sb[:].rearrange("k (p j) -> k j p", j=PACK)
-            h_ps = [
-                psum_start.tile([P, 2, BATCH], F32, name="h_ps0"),
-                psum_start.tile([P, 2, BATCH], F32, name="h_ps1"),
-            ]
-            for j in range(PACK):
-                nc.tensor.matmul(
-                    out=h_ps[j // 2][:, j % 2, :], lhsT=w1_by_j[:, j, :], rhs=cond_t[:], start=True, stop=True
-                )
-            for j in range(PACK):
-                nc.scalar.activation(
-                    out=h_grouped[:, :, j],
-                    in_=h_ps[j // 2][:, j % 2, :],
-                    func=ACT.Relu,
-                    bias=b1_f[:, j : j + 1],
-                    scale=1.0,
-                )
-            nc.vector.quantize_mx(
-                out=h_codes[:].bitcast(FP8X4),
-                scales=h_scales[:],
-                in_=h_grouped[:].rearrange("p b j -> p (b j)"),
-            )
-
-            bias_t_ps = psum_start.tile([P, 2 * P], BF16)
-            nc.tensor.transpose(bias_t_ps[:, 0:P], b2_rows_a[:], ident[:])
-            nc.tensor.transpose(bias_t_ps[:, P : 2 * P], b2_rows_b[:], ident[:])
-            nc.vector.tensor_copy(
-                out=bias_t[:].rearrange("p s c -> p (s c)"), in_=bias_t_ps[:, 0 : SECTIONS * TILES]
-            )
-            nc.vector.tensor_scalar_add(out=bias_t[:, 1, :], in0=bias_t[:, 1, :], scalar1=1.0)
-
-            pick_ps = psum_start.tile([P, P], BF16)
-            nc.tensor.transpose(pick_ps[:], pick_t[:], ident[:])
-            nc.vector.tensor_copy(out=pick[:], in_=pick_ps[:, 0:WIDE])
-
-        psum = ctx.enter_context(tc.psum_pool(name="psum", bufs=2))
-        psum_one = ctx.enter_context(tc.psum_pool(name="psum_one", bufs=1))
+        table_loaded = const.tile([P, 1], F32)
 
         grouped_mat2 = const.tile([P, 2, P, PACK], BF16, align_bytes=64)
-        nc.gpsimd.memset(grouped_mat2[:, :, PAIR_COLS:P, :], 0.0)
 
         w2_by_p = W2.rearrange("(p j) c -> p j c", j=PACK)
-
-        sums = [
-            psum_one.tile([P, HALVES, DIM + WIDE - 2], F32, name="sums_num"),
-            psum_one.tile([P, HALVES, DIM + WIDE - 2], F32, name="sums_den"),
-        ]
 
         tail_raw = const.tile([P, PACK, 3 * DIM], BF16)
         tail_grouped = const.tile([P, 3 * DIM, PACK], BF16, align_bytes=64)
         tail_codes = const.tile([P, 3 * DIM], U32, align_bytes=64)
         tail_scales = const.tile([P, 3 * DIM], U8, align_bytes=64)
         tail = const.tile([P, HALVES, 3, DIM], F32)
+        exp_alpha = const.tile([P, HALVES, DIM], F32)
+        exp_minus_alpha = const.tile([P, HALVES, DIM], F32)
+        gate_den = const.tile([P, HALVES, DIM], F32)
+        base = const.tile([P, HALVES, DIM], F32)
+        divisor = const.tile([P, HALVES, DIM], F32)
+        result = const.tile([P, HALVES, DIM], F32)
 
         x_e = const.tile([P, TILES, BATCH // 2], F32)
 
@@ -185,17 +108,22 @@ def tile_cn_pa_kernel(tc, x, cond, W1, b1, W2, b2, out):
         mat2_of, z1_of, m1m2_of, ez_of, elu1_of, num_of, den_of = [], [], [], [], [], [], []
 
         def regroup_on_scalar(n):
-            grouped = grouped_pool.tile([P, 2, 2, P, PACK], BF16, name="grouped", align_bytes=64)
-            for s in range(2):
-                copy = nc.vector.tensor_copy if s == 1 and n < FILL_UNITS else nc.scalar.copy
-                for t in range(2):
-                    copy(
-                        out=grouped[:, s, t, :, :].rearrange("p (c i) j -> p c j i", i=RUN),
-                        in_=raw_of[n][:, s, :, t * PAIR_COLS : t * PAIR_COLS + P].rearrange(
-                            "p j (c i) -> p c j i", i=RUN
-                        ),
-                    )
-            grouped_of.append(grouped)
+            grouped_of.append(grouped_pool.tile([P, 2, 2, P, PACK], BF16, name="grouped", align_bytes=64))
+            regroup(nc.scalar.copy, n, 0)
+            if n >= FILL_UNITS:
+                regroup(nc.scalar.copy, n, 1)
+
+        def regroup_on_vector(n):
+            regroup(nc.vector.tensor_copy, n, 1)
+
+        def regroup(copy, n, s):
+            for t in range(2):
+                copy(
+                    out=grouped_of[n][:, s, t, :, :].rearrange("p (c i) j -> p c j i", i=RUN),
+                    in_=raw_of[n][:, s, :, t * PAIR_COLS : t * PAIR_COLS + P].rearrange(
+                        "p j (c i) -> p c j i", i=RUN
+                    ),
+                )
 
         def regroup_on_gpsimd(n):
             nc.gpsimd.tensor_scalar(
@@ -311,19 +239,28 @@ def tile_cn_pa_kernel(tc, x, cond, W1, b1, W2, b2, out):
             if 0 <= n < PAIRS:
                 stage(n, *tile_of_unit)
 
-        load(0)
-        nc.sync.dma_start(out=tail_raw[:], in_=w2_by_p[:, :, TAIL0 : TAIL0 + 3 * DIM])
-        nc.vector.tensor_copy(out=tail_grouped[:], in_=tail_raw[:].rearrange("p j w -> p w j"))
-        for i in range(3):
-            cols = slice(i * DIM, (i + 1) * DIM)
-            nc.vector.quantize_mx(
-                out=tail_codes[:, cols].bitcast(FP8X4),
-                scales=tail_scales[:, cols],
-                in_=tail_grouped[:, cols, :].rearrange("p w j -> p (w j)"),
-            )
-        for h in range(HALVES):
+
+        def tail_load():
+            nc.sync.dma_start(out=tail_raw[:], in_=w2_by_p[:, :, TAIL0 : TAIL0 + 3 * DIM])
+            nc.sync.dma_start(out=b2_tail[:], in_=b2[TAIL0 : TAIL0 + 3 * DIM].partition_broadcast(P))
+
+        def tail_regroup():
+            nc.scalar.copy(out=tail_grouped[:], in_=tail_raw[:].rearrange("p j w -> p w j"))
+
+        def tail_quantise():
+            for i in range(3):
+                cols = slice(i * DIM, (i + 1) * DIM)
+                nc.vector.quantize_mx(
+                    out=tail_codes[:, cols].bitcast(FP8X4),
+                    scales=tail_scales[:, cols],
+                    in_=tail_grouped[:, cols, :].rearrange("p w j -> p (w j)"),
+                )
+
+        tail_ps_of = []
+
+        def tail_multiply(h):
             samples = slice(h * P, (h + 1) * P)
-            tail_ps = psum.tile([P, 3, DIM], F32, name="tail_ps", tag="p_ps0")
+            tail_ps = psum.tile([P, 3, DIM], F32, name="tail_ps", tag="p_ps2")
             for i in range(3):
                 cols = slice(i * DIM, (i + 1) * DIM)
                 nc.tensor.matmul_mx(
@@ -335,60 +272,170 @@ def tile_cn_pa_kernel(tc, x, cond, W1, b1, W2, b2, out):
                     start=True,
                     stop=True,
                 )
+            tail_ps_of.append(tail_ps)
+
+        def tail_add_bias(h):
             nc.vector.tensor_tensor(
                 out=tail[:, h, :, :].rearrange("p i d -> p (i d)"),
-                in0=tail_ps[:].rearrange("p i d -> p (i d)"),
+                in0=tail_ps_of[h][:].rearrange("p i d -> p (i d)"),
                 in1=b2_tail[:],
                 op=ALU.add,
             )
-        exp_alpha = const.tile([P, HALVES, DIM], F32)
-        exp_minus_alpha = const.tile([P, HALVES, DIM], F32)
-        gate_den = const.tile([P, HALVES, DIM], F32)
-        base = const.tile([P, HALVES, DIM], F32)
-        nc.scalar.activation(out=exp_alpha[:], in_=tail[:, :, 2, :], func=ACT.Exp, scale=0.1)
-        nc.scalar.activation(out=exp_minus_alpha[:], in_=tail[:, :, 2, :], func=ACT.Exp, scale=-0.1)
-        nc.scalar.activation(out=gate_den[:], in_=tail[:, :, 1, :], func=ACT.Exp, scale=-0.1)
-        nc.vector.tensor_tensor(out=base[:], in0=exp_alpha[:], in1=x_f[:], op=ALU.mult)
-        nc.vector.scalar_tensor_tensor(
-            out=gate_den[:], in0=gate_den[:], scalar=1.0, in1=exp_minus_alpha[:], op0=ALU.add, op1=ALU.mult
-        )
-        nc.vector.tensor_tensor(out=base[:], in0=base[:], in1=tail[:, :, 0, :], op=ALU.add)
-        nc.vector.tensor_scalar_mul(out=gate_den[:], in0=gate_den[:], scalar1=1.25)
-        divisor = const.tile([P, HALVES, DIM], F32)
-        result = const.tile([P, HALVES, DIM], F32)
 
-        for n in range(1, LOAD_AHEAD):
-            load(n)
+        def tail_on_scalar():
+            nc.scalar.activation(out=exp_alpha[:], in_=tail[:, :, 2, :], func=ACT.Exp, scale=0.1)
+            nc.scalar.activation(out=exp_minus_alpha[:], in_=tail[:, :, 2, :], func=ACT.Exp, scale=-0.1)
+            nc.scalar.activation(out=gate_den[:], in_=tail[:, :, 1, :], func=ACT.Exp, scale=-0.1)
 
-        with tc.manual_schedule():
-            for step in range(PAIRS + 8):
-                run(load, step + LOAD_AHEAD)
-                if (step + 1) % (X_CHUNK // 2) == 0 or step == 0:
-                    chunk = (step + 1) // (X_CHUNK // 2)
-                    if chunk < TILES // X_CHUNK:
-                        load_x(chunk)
-                for u in range(2):
-                    run(multiply, step - 2, u)
-                wide = WIDE_BESIDE_MX if step - 2 < PAIRS else WIDE
-                for u in range(2):
-                    run(add_up, step - 5, u, 1, wide)
-                    run(add_up, step - 7, u, 0, wide)
-                run(regroup_on_scalar, step)
+        def tail_on_vector():
+            nc.vector.tensor_tensor(out=base[:], in0=exp_alpha[:], in1=x_f[:], op=ALU.mult)
+            nc.vector.scalar_tensor_tensor(
+                out=gate_den[:], in0=gate_den[:], scalar=1.0, in1=exp_minus_alpha[:], op0=ALU.add, op1=ALU.mult
+            )
+            nc.vector.tensor_tensor(out=base[:], in0=base[:], in1=tail[:, :, 0, :], op=ALU.add)
+            nc.vector.tensor_scalar_mul(out=gate_den[:], in0=gate_den[:], scalar1=1.25)
+
+        def pipeline_step(step):
+            run(load, step + LOAD_AHEAD)
+            if step % 4 == 1:
+                run_chunk = (step + 3) // 4
+                if run_chunk < TILES // X_CHUNK:
+                    load_x(run_chunk)
+            if step == TAIL_STEP - 2 - LOAD_AHEAD:
+                tail_load()
+            for h in range(HALVES):
+                if step == TAIL_STEP + 3 + h:
+                    tail_add_bias(h)
+            for u in range(2):
+                run(multiply, step - 2, u)
+            for h in range(HALVES):
+                if step == TAIL_STEP + 2 + h:
+                    tail_multiply(h)
+            wide = WIDE_BESIDE_MX if step - 2 < PAIRS else WIDE
+            for u in range(2):
+                run(add_up, step - 5, u, 1, wide)
+                run(add_up, step - 7, u, 0, wide)
+            if step < EARLY_STEPS:
                 run(fetch, step - 2)
-                run(den_terms, step - 4)
-                run(exponential, step - 4)
-                run(quantise_mat1_bias1, step - 1)
-                run(quantise_mat2, step - 1)
-                run(regroup_on_gpsimd, step)
-                run(products, step - 3)
-                run(num_terms, step - 6)
-                run(elu_plus_one, step - 5)
-                if step == PAIRS - 1 + 6:
-                    nc.vector.scalar_tensor_tensor(
-                        out=divisor[:], in0=sums[1][:, :, 0:DIM], scalar=1.0, in1=gate_den[:],
-                        op0=ALU.add, op1=ALU.mult,
-                    )
-                    nc.vector.reciprocal(out=divisor[:], in_=divisor[:])
+            run(regroup_on_scalar, step)
+            if step >= EARLY_STEPS:
+                run(fetch, step - 2)
+            if step == TAIL_STEP:
+                tail_regroup()
+            run(den_terms, step - 4)
+            run(exponential, step - 4)
+            if step == TAIL_STEP + 5:
+                tail_on_scalar()
+            run(quantise_mat1_bias1, step - 1)
+            run(quantise_mat2, step - 1)
+            run(regroup_on_gpsimd, step)
+            run(products, step - 3)
+            run(num_terms, step - 6)
+            run(elu_plus_one, step - 5)
+            if step < FILL_UNITS:
+                regroup_on_vector(step)
+            if step == TAIL_STEP + 1:
+                tail_quantise()
+            if step == TAIL_STEP + 6:
+                tail_on_vector()
+            if step == PAIRS - 1 + 6:
+                nc.vector.scalar_tensor_tensor(
+                    out=divisor[:], in0=sums[1][:, :, 0:DIM], scalar=1.0, in1=gate_den[:], op0=ALU.add, op1=ALU.mult
+                )
+                nc.vector.reciprocal(out=divisor[:], in_=divisor[:])
+
+        nc.gpsimd.memset(minus_one[:], -1.0)
+        nc.gpsimd.memset(b2_rows_a[:], 0.0)
+        nc.gpsimd.memset(b2_rows_b[:], 0.0)
+        make_identity(nc, ident[:])
+        with nc.allow_non_contiguous_dma(reason="small inputs, loaded once"):
+            nc.sync.dma_start(out=cond_sb[:], in_=cond.rearrange("(h p) d -> p h d", p=P))
+            nc.sync.dma_start(out=w1_sb[:], in_=W1)
+            nc.sync.dma_start(out=b1_sb[:], in_=b1.rearrange("(p j) -> p j", j=PACK))
+            nc.sync.dma_start(out=x_sb[:], in_=x.rearrange("(h p) d -> p h d", p=P))
+            load(0)
+            nc.sync.dma_start(
+                out=b2_rows_a[:, 0:PAIR_COLS],
+                in_=b2[0 : P * PAIR_COLS].rearrange("(r m) -> r m", m=PAIR_COLS),
+            )
+            nc.sync.dma_start(
+                out=b2_rows_b[0:TILES, 0:PAIR_COLS],
+                in_=b2[P * PAIR_COLS : TAIL0].rearrange("(r m) -> r m", m=PAIR_COLS),
+            )
+        load(1)
+        nc.scalar.activation(out=table_loaded[:], in_=minus_one[:], func=ACT.Exp)
+        nc.gpsimd.memset(pick_t[:, PAIR_COLS:P], 0.0)
+        nc.gpsimd.tensor_scalar(
+            out=pick_t[:, 0:PAIR_COLS].rearrange("p (d l) -> p d l", l=LS),
+            in0=ident[:, 0:2].unsqueeze(2).to_broadcast([P, 2, LS]),
+            scalar1=1.0,
+            scalar2=0.0,
+            op0=ALU.mult,
+            op1=ALU.add,
+        )
+        nc.gpsimd.memset(grouped_mat2[:, :, PAIR_COLS:P, :], 0.0)
+
+        with tc.psum_pool(name="psum_start", bufs=1) as psum_start:
+            cond_t_ps = psum_start.tile([P, BATCH], BF16)
+            x_t_ps = psum_start.tile([P, BATCH], BF16)
+            for h in range(HALVES):
+                nc.tensor.transpose(cond_t_ps[:, h * P : (h + 1) * P], cond_sb[:, h, :], ident[:])
+            nc.scalar.copy(out=cond_t[:], in_=cond_t_ps[:])
+            for h in range(HALVES):
+                nc.tensor.transpose(x_t_ps[:, h * P : (h + 1) * P], x_sb[:, h, :], ident[:])
+            nc.scalar.copy(out=x_t[:], in_=x_t_ps[:])
+            nc.sync.dma_start(out=out[0:DIM, :], in_=x_t[:].bitcast(F32))
+            load(2)
+            load_x(0)
+            load(3)
+
+            nc.vector.tensor_copy(out=b1_f[:], in_=b1_sb[:])
+            w1_by_j = w1_sb[:].rearrange("k (p j) -> k j p", j=PACK)
+            h_ps = [
+                psum_start.tile([P, 2, BATCH], F32, name="h_ps0"),
+                psum_start.tile([P, 2, BATCH], F32, name="h_ps1"),
+            ]
+            for j in range(PACK):
+                nc.tensor.matmul(
+                    out=h_ps[j // 2][:, j % 2, :], lhsT=w1_by_j[:, j, :], rhs=cond_t[:], start=True, stop=True
+                )
+            for j in range(2):
+                nc.scalar.activation(
+                    out=h_grouped[:, :, j], in_=h_ps[0][:, j, :], func=ACT.Relu, bias=b1_f[:, j : j + 1], scale=1.0
+                )
+                nc.vector.tensor_scalar(
+                    out=h_grouped[:, :, 2 + j], in0=h_ps[1][:, j, :], scalar1=b1_f[:, 2 + j : 3 + j], scalar2=0.0,
+                    op0=ALU.add, op1=ALU.max,
+                )
+            nc.vector.quantize_mx(
+                out=h_codes[:].bitcast(FP8X4),
+                scales=h_scales[:],
+                in_=h_grouped[:].rearrange("p b j -> p (b j)"),
+            )
+
+            pipeline_step(0)
+
+            bias_t_ps = psum_start.tile([P, 2 * P], BF16)
+            nc.tensor.transpose(bias_t_ps[:, 0:P], b2_rows_a[:], ident[:])
+            nc.tensor.transpose(bias_t_ps[:, P : 2 * P], b2_rows_b[:], ident[:])
+            nc.vector.tensor_copy(
+                out=bias_t[:].rearrange("p s c -> p (s c)"), in_=bias_t_ps[:, 0 : SECTIONS * TILES]
+            )
+            pick_ps = psum_start.tile([P, P], BF16)
+            nc.tensor.transpose(pick_ps[:], pick_t[:], ident[:])
+            nc.vector.tensor_copy(out=pick[:], in_=pick_ps[:, 0:WIDE])
+            nc.vector.tensor_scalar_add(out=bias_t[:, 1, :], in0=bias_t[:, 1, :], scalar1=1.0)
+            nc.vector.tensor_copy(out=x_f[:], in_=x_sb[:])
+
+        psum = ctx.enter_context(tc.psum_pool(name="psum", bufs=2))
+        psum_one = ctx.enter_context(tc.psum_pool(name="psum_one", bufs=1))
+        sums = [
+            psum_one.tile([P, HALVES, DIM + WIDE - 2], F32, name="sums_num"),
+            psum_one.tile([P, HALVES, DIM + WIDE - 2], F32, name="sums_den"),
+        ]
+
+        for step in range(1, PAIRS + 8):
+            pipeline_step(step)
 
         nc.vector.tensor_tensor(out=result[:], in0=sums[0][:, :, 0:DIM], in1=divisor[:], op=ALU.mult)
         nc.vector.tensor_tensor(out=result[:], in0=result[:], in1=base[:], op=ALU.add)

@@ -98,7 +98,7 @@ def tile_cn_pa_kernel(tc, x, cond, W1, b1, W2, b2, out):
 
         def load(n):
             raw = raw_pool.tile([P, SECTIONS, PACK, 2 * P], BF16, name="raw")
-            width = STEP_COLS + SPARE
+            width = 2 * P
             for s in range(SECTIONS):
                 col0 = s * DL + n * STEP_COLS
                 nc.sync.dma_start(out=raw[:, s, :, 0:width], in_=w2_by_p[:, :, col0 : col0 + width])

@@ -33,8 +33,7 @@ WIDE = 64
 WIDE_BESIDE_MX = 48
 X_CHUNK = 8
 TAIL_STEP = 12
-EARLY_STEPS = 6
-FILL_UNITS = 3
+FILL_UNITS = 6
 
 FLOPS = 2 * BATCH * DIM * HID + 2 * BATCH * HID * (TAIL0 + 3 * DIM)
 
@@ -315,27 +314,24 @@ def tile_cn_pa_kernel(tc, x, cond, W1, b1, W2, b2, out):
             for u in range(2):
                 run(add_up, step - 5, u, 1, wide)
                 run(add_up, step - 7, u, 0, wide)
-            if step < EARLY_STEPS:
-                run(fetch, step - 2)
             run(regroup_on_scalar, step)
-            if step >= EARLY_STEPS:
-                run(fetch, step - 2)
+            run(fetch, step - 2)
             if step == TAIL_STEP:
                 tail_regroup()
             run(den_terms, step - 4)
             run(exponential, step - 4)
             if step == TAIL_STEP + 5:
                 tail_on_scalar()
-            run(quantise_mat1_bias1, step - 1)
-            run(quantise_mat2, step - 1)
-            run(regroup_on_gpsimd, step)
             run(products, step - 3)
             run(num_terms, step - 6)
             run(elu_plus_one, step - 5)
-            if step < FILL_UNITS:
-                regroup_on_vector(step)
             if step == TAIL_STEP + 1:
                 tail_quantise()
+            if step < FILL_UNITS:
+                regroup_on_vector(step)
+            run(quantise_mat1_bias1, step - 1)
+            run(quantise_mat2, step - 1)
+            run(regroup_on_gpsimd, step)
             if step == TAIL_STEP + 6:
                 tail_on_vector()
             if step == PAIRS - 1 + 6:

@@ -26,7 +26,7 @@ TILES = DIM // 2
 PAIRS = TILES // 2
 STEP_COLS = 2 * PAIR_COLS
 SPARE = P - PAIR_COLS
-RUN = 4
+RUN = 2
 LOAD_AHEAD = 4
 GROUPED_BUFS = 3
 WIDE = 64

@@ -43,7 +43,6 @@ def tile_cn_pa_kernel(tc, x, cond, W1, b1, W2, b2, out):
     with ExitStack() as ctx:
         const = ctx.enter_context(tc.tile_pool(name="const", bufs=1))
         raw_pool = ctx.enter_context(tc.tile_pool(name="raw", bufs=LOAD_AHEAD + 1))
-        grouped_pool = ctx.enter_context(tc.tile_pool(name="grouped", bufs=GROUPED_BUFS))
         mx_pool = ctx.enter_context(tc.tile_pool(name="mx", bufs=3))
         work = ctx.enter_context(tc.tile_pool(name="work", bufs=3))
         ctx.enter_context(tc.manual_schedule())
@@ -68,6 +67,8 @@ def tile_cn_pa_kernel(tc, x, cond, W1, b1, W2, b2, out):
         h_scales = const.tile([P, BATCH], U8, align_bytes=64)
         minus_one = const.tile([P, 1], F32)
         table_loaded = const.tile([P, 1], F32)
+
+        grouped = const.tile([P, GROUPED_BUFS, 2, 2, P, PACK], BF16, align_bytes=64)
 
         grouped_mat2 = const.tile([P, 2, P, PACK], BF16, align_bytes=64)
 
@@ -103,23 +104,22 @@ def tile_cn_pa_kernel(tc, x, cond, W1, b1, W2, b2, out):
                 nc.sync.dma_start(out=raw[:, s, :, 0:width], in_=w2_by_p[:, :, col0 : col0 + width])
             raw_of.append(raw)
 
-        grouped_of, codes_of, scales_of, p_ps_of = [], [], [], []
+        codes_of, scales_of, p_ps_of = [], [], []
         mat2_of, z1_of, m1m2_of, ez_of, elu1_of, num_of, den_of = [], [], [], [], [], [], []
 
         def regroup_on_scalar(n):
-            grouped_of.append(grouped_pool.tile([P, 2, 2, P, PACK], BF16, name="grouped", align_bytes=64))
-            regroup(nc.scalar.copy, n, 0)
+            regroup(nc.scalar.copy, n, 0, PAIR_COLS)
             if n >= FILL_UNITS:
-                regroup(nc.scalar.copy, n, 1)
+                regroup(nc.scalar.copy, n, 1, PAIR_COLS)
 
         def regroup_on_vector(n):
-            regroup(nc.vector.tensor_copy, n, 1)
+            regroup(nc.vector.tensor_copy, n, 1, P)
 
-        def regroup(copy, n, s):
+        def regroup(copy, n, s, width):
             for t in range(2):
                 copy(
-                    out=grouped_of[n][:, s, t, :, :].rearrange("p (c i) j -> p c j i", i=RUN),
-                    in_=raw_of[n][:, s, :, t * PAIR_COLS : t * PAIR_COLS + P].rearrange(
+                    out=grouped[:, n % GROUPED_BUFS, s, t, 0:width, :].rearrange("p (c i) j -> p c j i", i=RUN),
+                    in_=raw_of[n][:, s, :, t * PAIR_COLS : t * PAIR_COLS + width].rearrange(
                         "p j (c i) -> p c j i", i=RUN
                     ),
                 )
@@ -137,7 +137,7 @@ def tile_cn_pa_kernel(tc, x, cond, W1, b1, W2, b2, out):
             nc.vector.quantize_mx(
                 out=codes[:, 0:2, :].rearrange("p s w -> p (s w)").bitcast(FP8X4),
                 scales=scales[:, 0:2, :].rearrange("p s w -> p (s w)"),
-                in_=grouped_of[n][:].rearrange("p s t w j -> p (s t w j)"),
+                in_=grouped[:, n % GROUPED_BUFS, :, :, :, :].rearrange("p s t w j -> p (s t w j)"),
             )
             codes_of.append(codes)
             scales_of.append(scales)
@@ -165,7 +165,7 @@ def tile_cn_pa_kernel(tc, x, cond, W1, b1, W2, b2, out):
                 )
 
         def fetch(n):
-            mat2 = work.tile([P, 2, BATCH], F32, name="mat2", bufs=5)
+            mat2 = work.tile([P, 2, BATCH], F32, name="mat2", bufs=4)
             for u in range(2):
                 c = 2 * n + u
                 nc.scalar.activation(
@@ -244,7 +244,10 @@ def tile_cn_pa_kernel(tc, x, cond, W1, b1, W2, b2, out):
             nc.sync.dma_start(out=b2_tail[:], in_=b2[TAIL0 : TAIL0 + 3 * DIM].partition_broadcast(P))
 
         def tail_regroup():
-            nc.scalar.copy(out=tail_grouped[:], in_=tail_raw[:].rearrange("p j w -> p w j"))
+            nc.scalar.copy(
+                out=tail_grouped[:].rearrange("p (c i) j -> p c j i", i=RUN),
+                in_=tail_raw[:].rearrange("p j (c i) -> p c j i", i=RUN),
+            )
 
         def tail_quantise():
             for i in range(3):
@@ -312,19 +315,19 @@ def tile_cn_pa_kernel(tc, x, cond, W1, b1, W2, b2, out):
                     tail_multiply(h)
             wide = WIDE_BESIDE_MX if step - 2 < PAIRS else WIDE
             for u in range(2):
-                run(add_up, step - 5, u, 1, wide)
-                run(add_up, step - 7, u, 0, wide)
+                run(add_up, step - 4, u, 1, wide)
+                run(add_up, step - 6, u, 0, wide)
             run(regroup_on_scalar, step)
             run(fetch, step - 2)
             if step == TAIL_STEP:
                 tail_regroup()
-            run(den_terms, step - 4)
-            run(exponential, step - 4)
+            run(products, step - 3)
+            run(den_terms, step - 3)
+            run(exponential, step - 3)
             if step == TAIL_STEP + 5:
                 tail_on_scalar()
-            run(products, step - 3)
-            run(num_terms, step - 6)
-            run(elu_plus_one, step - 5)
+            run(num_terms, step - 5)
+            run(elu_plus_one, step - 4)
             if step == TAIL_STEP + 1:
                 tail_quantise()
             if step < FILL_UNITS:
@@ -334,7 +337,7 @@ def tile_cn_pa_kernel(tc, x, cond, W1, b1, W2, b2, out):
             run(regroup_on_gpsimd, step)
             if step == TAIL_STEP + 6:
                 tail_on_vector()
-            if step == PAIRS - 1 + 6:
+            if step == PAIRS - 1 + 5:
                 nc.vector.scalar_tensor_tensor(
                     out=divisor[:], in0=sums[1][:, :, 0:DIM], scalar=1.0, in1=gate_den[:], op0=ALU.add, op1=ALU.mult
                 )
@@ -370,6 +373,7 @@ def tile_cn_pa_kernel(tc, x, cond, W1, b1, W2, b2, out):
             op1=ALU.add,
         )
         nc.gpsimd.memset(grouped_mat2[:, :, PAIR_COLS:P, :], 0.0)
+        nc.gpsimd.memset(grouped[:, :, :, :, PAIR_COLS:P, :].rearrange("p b s t w j -> p (b s t) (w j)"), 0.0)
 
         with tc.psum_pool(name="psum_start", bufs=1) as psum_start:
             cond_t_ps = psum_start.tile([P, BATCH], BF16)
@@ -430,7 +434,7 @@ def tile_cn_pa_kernel(tc, x, cond, W1, b1, W2, b2, out):
             psum_one.tile([P, HALVES, DIM + WIDE - 2], F32, name="sums_den"),
         ]
 
-        for step in range(1, PAIRS + 8):
+        for step in range(1, PAIRS + 6):
             pipeline_step(step)
 
         nc.vector.tensor_tensor(out=result[:], in0=sums[0][:, :, 0:DIM], in1=divisor[:], op=ALU.mult)

@@ -132,17 +132,16 @@ def tile_cn_pa_kernel(tc, x, cond, W1, b1, W2, b2, out):
             )
 
         def quantise_mat1_bias1(n):
-            codes = mx_pool.tile([P, SECTIONS, 2 * P], U32, name="codes", align_bytes=64)
-            scales = mx_pool.tile([P, SECTIONS, 2 * P], U8, name="scales", align_bytes=64)
+            codes, scales = codes_of[n], scales_of[n]
             nc.vector.quantize_mx(
                 out=codes[:, 0:2, :].rearrange("p s w -> p (s w)").bitcast(FP8X4),
                 scales=scales[:, 0:2, :].rearrange("p s w -> p (s w)"),
                 in_=grouped[:, n % GROUPED_BUFS, :, :, :, :].rearrange("p s t w j -> p (s t w j)"),
             )
-            codes_of.append(codes)
-            scales_of.append(scales)
 
         def quantise_mat2(n):
+            codes_of.append(mx_pool.tile([P, SECTIONS, 2 * P], U32, name="codes", align_bytes=64))
+            scales_of.append(mx_pool.tile([P, SECTIONS, 2 * P], U8, name="scales", align_bytes=64))
             nc.vector.quantize_mx(
                 out=codes_of[n][:, 2, :].bitcast(FP8X4),
                 scales=scales_of[n][:, 2, :],
@@ -332,8 +331,8 @@ def tile_cn_pa_kernel(tc, x, cond, W1, b1, W2, b2, out):
                 tail_quantise()
             if step < FILL_UNITS:
                 regroup_on_vector(step)
-            run(quantise_mat1_bias1, step - 1)
             run(quantise_mat2, step - 1)
+            run(quantise_mat1_bias1, step - 1)
             run(regroup_on_gpsimd, step)
             if step == TAIL_STEP + 6:
                 tail_on_vector()

from contextlib import ExitStack

import concourse.mybir as mybir
from concourse.masks import make_identity

F32 = mybir.dt.float32
BF16 = mybir.dt.bfloat16
U32 = mybir.dt.uint32
U8 = mybir.dt.uint8
FP8X4 = mybir.dt.float8_e4m3fn_x4
ALU = mybir.AluOpType
ACT = mybir.ActivationFunctionType

P = 128
PACK = 4
BATCH = 256
HALVES = BATCH // P
DIM = 128
HID = 512
LS = 63
DL = DIM * LS
SECTIONS = 3
TAIL0 = SECTIONS * DL
PAIR_COLS = 2 * LS
TILES = DIM // 2
PAIRS = TILES // 2
STEP_COLS = 2 * PAIR_COLS
SPARE = P - PAIR_COLS
RUN = 2
LOAD_AHEAD = 4
GROUPED_BUFS = 3
WIDE = 64
WIDE_BESIDE_MX = 48
X_CHUNK = 8
TAIL_STEP = 12
FILL_UNITS = 6

FLOPS = 2 * BATCH * DIM * HID + 2 * BATCH * HID * (TAIL0 + 3 * DIM)


def tile_cn_pa_kernel(tc, x, cond, W1, b1, W2, b2, out):
    nc = tc.nc
    with ExitStack() as ctx:
        const = ctx.enter_context(tc.tile_pool(name="const", bufs=1))
        raw_pool = ctx.enter_context(tc.tile_pool(name="raw", bufs=LOAD_AHEAD + 1))
        mx_pool = ctx.enter_context(tc.tile_pool(name="mx", bufs=3))
        work = ctx.enter_context(tc.tile_pool(name="work", bufs=3))
        ctx.enter_context(tc.manual_schedule())

        x_sb = const.tile([P, HALVES, DIM], BF16)
        cond_sb = const.tile([P, HALVES, DIM], BF16)
        w1_sb = const.tile([P, HID], BF16)
        b1_sb = const.tile([P, PACK], BF16)
        b2_rows_a = const.tile([P, P], BF16)
        b2_rows_b = const.tile([P, P], BF16)
        b2_tail = const.tile([P, 3 * DIM], BF16)
        ident = const.tile([P, P], BF16)
        pick_t = const.tile([P, P], BF16)
        x_t = const.tile([P, BATCH], BF16)
        cond_t = const.tile([P, BATCH], BF16)
        bias_t = const.tile([P, SECTIONS, TILES], F32)
        pick = const.tile([P, WIDE], F32)
        b1_f = const.tile([P, PACK], F32)
        x_f = const.tile([P, HALVES, DIM], F32)
        h_grouped = const.tile([P, BATCH, PACK], BF16, align_bytes=64)
        h_codes = const.tile([P, BATCH], U32, align_bytes=64)
        h_scales = const.tile([P, BATCH], U8, align_bytes=64)
        minus_one = const.tile([P, 1], F32)
        table_loaded = const.tile([P, 1], F32)

        grouped = const.tile([P, GROUPED_BUFS, 2, 2, P, PACK], BF16, align_bytes=64)

        grouped_mat2 = const.tile([P, 2, P, PACK], BF16, align_bytes=64)

        w2_by_p = W2.rearrange("(p j) c -> p j c", j=PACK)

        tail_raw = const.tile([P, PACK, 3 * DIM], BF16)
        tail_grouped = const.tile([P, 3 * DIM, PACK], BF16, align_bytes=64)
        tail_codes = const.tile([P, 3 * DIM], U32, align_bytes=64)
        tail_scales = const.tile([P, 3 * DIM], U8, align_bytes=64)
        tail = const.tile([P, HALVES, 3, DIM], F32)
        exp_alpha = const.tile([P, HALVES, DIM], F32)
        exp_minus_alpha = const.tile([P, HALVES, DIM], F32)
        gate_den = const.tile([P, HALVES, DIM], F32)
        base = const.tile([P, HALVES, DIM], F32)
        divisor = const.tile([P, HALVES, DIM], F32)
        result = const.tile([P, HALVES, DIM], F32)

        x_e = const.tile([P, TILES, BATCH // 2], F32)

        def load_x(chunk):
            tiles = slice(chunk * X_CHUNK, (chunk + 1) * X_CHUNK)
            for e, parts in enumerate((slice(0, LS), slice(LS, P))):
                rows = out[2 * tiles.start + e : 2 * tiles.stop : 2, :]
                nc.sync.dma_start(out=x_e[parts, tiles, :], in_=rows.partition_broadcast(parts.stop - parts.start))

        raw_of = []

        def load(n):
            raw = raw_pool.tile([P, SECTIONS, PACK, 2 * P], BF16, name="raw")
            width = 2 * P
            for s in range(SECTIONS):
                col0 = s * DL + n * STEP_COLS
                nc.sync.dma_start(out=raw[:, s, :, 0:width], in_=w2_by_p[:, :, col0 : col0 + width])
            raw_of.append(raw)

        codes_of, scales_of, p_ps_of = [], [], []
        mat2_of, z1_of, m1m2_of, ez_of, elu1_of, num_of, den_of = [], [], [], [], [], [], []

        def regroup_on_scalar(n):
            regroup(nc.scalar.copy, n, 0, PAIR_COLS)
            if n >= FILL_UNITS:
                regroup(nc.scalar.copy, n, 1, PAIR_COLS)

        def regroup_on_vector(n):
            regroup(nc.vector.tensor_copy, n, 1, P)

        def regroup(copy, n, s, width):
            for t in range(2):
                copy(
                    out=grouped[:, n % GROUPED_BUFS, s, t, 0:width, :].rearrange("p (c i) j -> p c j i", i=RUN),
                    in_=raw_of[n][:, s, :, t * PAIR_COLS : t * PAIR_COLS + width].rearrange(
                        "p j (c i) -> p c j i", i=RUN
                    ),
                )

        def regroup_on_gpsimd(n):
            nc.gpsimd.tensor_scalar(
                out=grouped_mat2[:, :, 0:PAIR_COLS, :],
                in0=raw_of[n][:, 2, :, 0:STEP_COLS].rearrange("p j (t w) -> p t w j", t=2),
                scalar1=1.0, scalar2=0.0, op0=ALU.mult, op1=ALU.add,
            )

        def quantise_mat1_bias1(n):
            codes, scales = codes_of[n], scales_of[n]
            nc.vector.quantize_mx(
                out=codes[:, 0:2, :].rearrange("p s w -> p (s w)").bitcast(FP8X4),
                scales=scales[:, 0:2, :].rearrange("p s w -> p (s w)"),
                in_=grouped[:, n % GROUPED_BUFS, :, :, :, :].rearrange("p s t w j -> p (s t w j)"),
            )

        def quantise_mat2(n):
            codes_of.append(mx_pool.tile([P, SECTIONS, 2 * P], U32, name="codes", align_bytes=64))
            scales_of.append(mx_pool.tile([P, SECTIONS, 2 * P], U8, name="scales", align_bytes=64))
            nc.vector.quantize_mx(
                out=codes_of[n][:, 2, :].bitcast(FP8X4),
                scales=scales_of[n][:, 2, :],
                in_=grouped_mat2[:].rearrange("p t w j -> p (t w j)"),
            )

        def multiply(n, u):
            if u == 0:
                p_ps_of.append([psum.tile([P, 2, BATCH], F32, name="p_ps%d" % s) for s in range(SECTIONS)])
            cols = slice(u * P, (u + 1) * P)
            for s in range(SECTIONS):
                nc.tensor.matmul_mx(
                    out=p_ps_of[n][s][:, u, :],
                    lhsT=codes_of[n][:, s, cols].bitcast(FP8X4),
                    lhsT_scale=scales_of[n][:, s, cols],
                    rhs=h_codes[:].bitcast(FP8X4),
                    rhs_scale=h_scales[:],
                    start=True,
                    stop=True,
                )

        def fetch(n):
            mat2 = work.tile([P, 2, BATCH], F32, name="mat2", bufs=4)
            for u in range(2):
                c = 2 * n + u
                nc.scalar.activation(
                    out=mat2[:, u, :], in_=p_ps_of[n][2][:, u, :], func=ACT.Identity,
                    bias=bias_t[:, 2, c : c + 1], scale=1.0,
                )
            mat2_of.append(mat2)

        def products(n):
            xm1 = work.tile([P, 2, BATCH], F32, name="xm1")
            z1 = work.tile([P, 2, BATCH], F32, name="z1")
            m1m2 = work.tile([P, 2, BATCH], F32, name="m1m2")
            p_ps = p_ps_of[n]
            bias = [bias_t[:, :, 2 * n + u : 2 * n + u + 1] for u in range(2)]
            for u in range(2):
                nc.vector.scalar_tensor_tensor(
                    out=m1m2[:, u, :], in0=p_ps[0][:, u, :], scalar=bias[u][:, 0, :],
                    in1=mat2_of[n][:, u, :], op0=ALU.add, op1=ALU.mult,
                )
            for u in range(2):
                nc.vector.scalar_tensor_tensor(
                    out=xm1[:, u, :], in0=p_ps[0][:, u, :], scalar=bias[u][:, 0, :],
                    in1=x_e[:, 2 * n + u, :].bitcast(BF16), op0=ALU.add, op1=ALU.mult,
                )
            for u in range(2):
                nc.vector.scalar_tensor_tensor(
                    out=z1[:, u, :], in0=p_ps[1][:, u, :], scalar=bias[u][:, 1, :],
                    in1=xm1[:, u, :], op0=ALU.add, op1=ALU.add,
                )
            z1_of.append(z1)
            m1m2_of.append(m1m2)

        def den_terms(n):
            terms = work.tile([P, 2, BATCH], F32, name="den_terms")
            nc.scalar.activation(out=terms[:], in_=m1m2_of[n][:], func=ACT.Relu, scale=-1.0)
            den_of.append(terms)

        def exponential(n):
            ez = work.tile([P, 2, BATCH], F32, name="ez")
            nc.scalar.activation(out=ez[:], in_=z1_of[n][:], func=ACT.Exp, bias=minus_one[:], scale=1.0)
            ez_of.append(ez)

        def elu_plus_one(n):
            elu1 = work.tile([P, 2, BATCH], F32, name="elu1")
            nc.vector.scalar_tensor_tensor(
                out=elu1[:], in0=ez_of[n][:], scalar=1.0, in1=z1_of[n][:], op0=ALU.min, op1=ALU.max
            )
            elu1_of.append(elu1)

        def num_terms(n):
            terms = work.tile([P, 2, BATCH], F32, name="num_terms")
            nc.vector.scalar_tensor_tensor(
                out=terms[:], in0=elu1_of[n][:], scalar=-1.0, in1=mat2_of[n][:], op0=ALU.add, op1=ALU.mult
            )
            num_of.append(terms)

        def add_up(n, u, kind, wide):
            c = 2 * n + u
            terms = (num_of, den_of)[kind][n]
            for h in range(HALVES):
                nc.tensor.matmul(
                    out=sums[kind][:, h, 2 * c : 2 * c + wide],
                    lhsT=terms[:, u, h * P : (h + 1) * P],
                    rhs=pick[:, 0:wide],
                    start=True,
                    stop=True,
                )

        def run(stage, n, *tile_of_unit):
            if 0 <= n < PAIRS:
                stage(n, *tile_of_unit)


        def tail_load():
            nc.sync.dma_start(out=tail_raw[:], in_=w2_by_p[:, :, TAIL0 : TAIL0 + 3 * DIM])
            nc.sync.dma_start(out=b2_tail[:], in_=b2[TAIL0 : TAIL0 + 3 * DIM].partition_broadcast(P))

        def tail_regroup():
            nc.scalar.copy(
                out=tail_grouped[:].rearrange("p (c i) j -> p c j i", i=RUN),
                in_=tail_raw[:].rearrange("p j (c i) -> p c j i", i=RUN),
            )

        def tail_quantise():
            for i in range(3):
                cols = slice(i * DIM, (i + 1) * DIM)
                nc.vector.quantize_mx(
                    out=tail_codes[:, cols].bitcast(FP8X4),
                    scales=tail_scales[:, cols],
                    in_=tail_grouped[:, cols, :].rearrange("p w j -> p (w j)"),
                )

        tail_ps_of = []

        def tail_multiply(h):
            samples = slice(h * P, (h + 1) * P)
            tail_ps = psum.tile([P, 3, DIM], F32, name="tail_ps", tag="p_ps2")
            for i in range(3):
                cols = slice(i * DIM, (i + 1) * DIM)
                nc.tensor.matmul_mx(
                    out=tail_ps[:, i, :],
                    lhsT=h_codes[:, samples].bitcast(FP8X4),
                    lhsT_scale=h_scales[:, samples],
                    rhs=tail_codes[:, cols].bitcast(FP8X4),
                    rhs_scale=tail_scales[:, cols],
                    start=True,
                    stop=True,
                )
            tail_ps_of.append(tail_ps)

        def tail_add_bias(h):
            nc.vector.tensor_tensor(
                out=tail[:, h, :, :].rearrange("p i d -> p (i d)"),
                in0=tail_ps_of[h][:].rearrange("p i d -> p (i d)"),
                in1=b2_tail[:],
                op=ALU.add,
            )

        def tail_on_scalar():
            nc.scalar.activation(out=exp_alpha[:], in_=tail[:, :, 2, :], func=ACT.Exp, scale=0.1)
            nc.scalar.activation(out=exp_minus_alpha[:], in_=tail[:, :, 2, :], func=ACT.Exp, scale=-0.1)
            nc.scalar.activation(out=gate_den[:], in_=tail[:, :, 1, :], func=ACT.Exp, scale=-0.1)

        def tail_on_vector():
            nc.vector.tensor_tensor(out=base[:], in0=exp_alpha[:], in1=x_f[:], op=ALU.mult)
            nc.vector.scalar_tensor_tensor(
                out=gate_den[:], in0=gate_den[:], scalar=1.0, in1=exp_minus_alpha[:], op0=ALU.add, op1=ALU.mult
            )
            nc.vector.tensor_tensor(out=base[:], in0=base[:], in1=tail[:, :, 0, :], op=ALU.add)
            nc.vector.tensor_scalar_mul(out=gate_den[:], in0=gate_den[:], scalar1=1.25)

        def pipeline_step(step):
            run(load, step + LOAD_AHEAD)
            if step % 4 == 1:
                run_chunk = (step + 3) // 4
                if run_chunk < TILES // X_CHUNK:
                    load_x(run_chunk)
            if step == TAIL_STEP - 2 - LOAD_AHEAD:
                tail_load()
            for h in range(HALVES):
                if step == TAIL_STEP + 3 + h:
                    tail_add_bias(h)
            for u in range(2):
                run(multiply, step - 2, u)
            for h in range(HALVES):
                if step == TAIL_STEP + 2 + h:
                    tail_multiply(h)
            wide = WIDE_BESIDE_MX if step - 2 < PAIRS else WIDE
            for u in range(2):
                run(add_up, step - 4, u, 1, wide)
                run(add_up, step - 6, u, 0, wide)
            run(regroup_on_scalar, step)
            run(fetch, step - 2)
            if step == TAIL_STEP:
                tail_regroup()
            run(products, step - 3)
            run(den_terms, step - 3)
            run(exponential, step - 3)
            if step == TAIL_STEP + 5:
                tail_on_scalar()
            run(num_terms, step - 5)
            run(elu_plus_one, step - 4)
            if step == TAIL_STEP + 1:
                tail_quantise()
            if step < FILL_UNITS:
                regroup_on_vector(step)
            run(quantise_mat2, step - 1)
            run(quantise_mat1_bias1, step - 1)
            run(regroup_on_gpsimd, step)
            if step == TAIL_STEP + 6:
                tail_on_vector()
            if step == PAIRS - 1 + 5:
                nc.vector.scalar_tensor_tensor(
                    out=divisor[:], in0=sums[1][:, :, 0:DIM], scalar=1.0, in1=gate_den[:], op0=ALU.add, op1=ALU.mult
                )
                nc.vector.reciprocal(out=divisor[:], in_=divisor[:])

        nc.gpsimd.memset(minus_one[:], -1.0)
        nc.gpsimd.memset(b2_rows_a[:], 0.0)
        nc.gpsimd.memset(b2_rows_b[:], 0.0)
        make_identity(nc, ident[:])
        with nc.allow_non_contiguous_dma(reason="small inputs, loaded once"):
            nc.sync.dma_start(out=cond_sb[:], in_=cond.rearrange("(h p) d -> p h d", p=P))
            nc.sync.dma_start(out=w1_sb[:], in_=W1)
            nc.sync.dma_start(out=b1_sb[:], in_=b1.rearrange("(p j) -> p j", j=PACK))
            nc.sync.dma_start(out=x_sb[:], in_=x.rearrange("(h p) d -> p h d", p=P))
            load(0)
            nc.sync.dma_start(
                out=b2_rows_a[:, 0:PAIR_COLS],
                in_=b2[0 : P * PAIR_COLS].rearrange("(r m) -> r m", m=PAIR_COLS),
            )
            nc.sync.dma_start(
                out=b2_rows_b[0:TILES, 0:PAIR_COLS],
                in_=b2[P * PAIR_COLS : TAIL0].rearrange("(r m) -> r m", m=PAIR_COLS),
            )
        load(1)
        nc.scalar.activation(out=table_loaded[:], in_=minus_one[:], func=ACT.Exp)
        nc.gpsimd.memset(pick_t[:, PAIR_COLS:P], 0.0)
        nc.gpsimd.tensor_scalar(
            out=pick_t[:, 0:PAIR_COLS].rearrange("p (d l) -> p d l", l=LS),
            in0=ident[:, 0:2].unsqueeze(2).to_broadcast([P, 2, LS]),
            scalar1=1.0,
            scalar2=0.0,
            op0=ALU.mult,
            op1=ALU.add,
        )
        nc.gpsimd.memset(grouped_mat2[:, :, PAIR_COLS:P, :], 0.0)
        nc.gpsimd.memset(grouped[:, :, :, :, PAIR_COLS:P, :].rearrange("p b s t w j -> p (b s t) (w j)"), 0.0)

        with tc.psum_pool(name="psum_start", bufs=1) as psum_start:
            cond_t_ps = psum_start.tile([P, BATCH], BF16)
            x_t_ps = psum_start.tile([P, BATCH], BF16)
            for h in range(HALVES):
                nc.tensor.transpose(cond_t_ps[:, h * P : (h + 1) * P], cond_sb[:, h, :], ident[:])
            nc.scalar.copy(out=cond_t[:], in_=cond_t_ps[:])
            for h in range(HALVES):
                nc.tensor.transpose(x_t_ps[:, h * P : (h + 1) * P], x_sb[:, h, :], ident[:])
            nc.scalar.copy(out=x_t[:], in_=x_t_ps[:])
            nc.sync.dma_start(out=out[0:DIM, :], in_=x_t[:].bitcast(F32))
            load(2)
            load_x(0)
            load(3)

            nc.vector.tensor_copy(out=b1_f[:], in_=b1_sb[:])
            w1_by_j = w1_sb[:].rearrange("k (p j) -> k j p", j=PACK)
            h_ps = [
                psum_start.tile([P, 2, BATCH], F32, name="h_ps0"),
                psum_start.tile([P, 2, BATCH], F32, name="h_ps1"),
            ]
            for j in range(PACK):
                nc.tensor.matmul(
                    out=h_ps[j // 2][:, j % 2, :], lhsT=w1_by_j[:, j, :], rhs=cond_t[:], start=True, stop=True
                )
            for j in range(2):
                nc.scalar.activation(
                    out=h_grouped[:, :, j], in_=h_ps[0][:, j, :], func=ACT.Relu, bias=b1_f[:, j : j + 1], scale=1.0
                )
                nc.vector.tensor_scalar(
                    out=h_grouped[:, :, 2 + j], in0=h_ps[1][:, j, :], scalar1=b1_f[:, 2 + j : 3 + j], scalar2=0.0,
                    op0=ALU.add, op1=ALU.max,
                )
            nc.vector.quantize_mx(
                out=h_codes[:].bitcast(FP8X4),
                scales=h_scales[:],
                in_=h_grouped[:].rearrange("p b j -> p (b j)"),
            )

            pipeline_step(0)

            bias_t_ps = psum_start.tile([P, 2 * P], BF16)
            nc.tensor.transpose(bias_t_ps[:, 0:P], b2_rows_a[:], ident[:])
            nc.tensor.transpose(bias_t_ps[:, P : 2 * P], b2_rows_b[:], ident[:])
            nc.vector.tensor_copy(
                out=bias_t[:].rearrange("p s c -> p (s c)"), in_=bias_t_ps[:, 0 : SECTIONS * TILES]
            )
            pick_ps = psum_start.tile([P, P], BF16)
            nc.tensor.transpose(pick_ps[:], pick_t[:], ident[:])
            nc.vector.tensor_copy(out=pick[:], in_=pick_ps[:, 0:WIDE])
            nc.vector.tensor_scalar_add(out=bias_t[:, 1, :], in0=bias_t[:, 1, :], scalar1=1.0)
            nc.vector.tensor_copy(out=x_f[:], in_=x_sb[:])

        psum = ctx.enter_context(tc.psum_pool(name="psum", bufs=2))
        psum_one = ctx.enter_context(tc.psum_pool(name="psum_one", bufs=1))
        sums = [
            psum_one.tile([P, HALVES, DIM + WIDE - 2], F32, name="sums_num"),
            psum_one.tile([P, HALVES, DIM + WIDE - 2], F32, name="sums_den"),
        ]

        for step in range(1, PAIRS + 6):
            pipeline_step(step)

        nc.vector.tensor_tensor(out=result[:], in0=sums[0][:, :, 0:DIM], in1=divisor[:], op=ALU.mult)
        nc.vector.tensor_tensor(out=result[:], in0=result[:], in1=base[:], op=ALU.add)
        nc.sync.dma_start(out=out.rearrange("(h p) d -> p h d", p=P), in_=result[:])
